import numpy as np
import ml_dtypes


def mxq(x, axis, fmt="e4m3"):
    dtype, down = {"e4m3": (ml_dtypes.float8_e4m3fn, 7), "e5m2": (ml_dtypes.float8_e5m2, 14)}[fmt]
    v = np.moveaxis(np.asarray(x, np.float32).astype(ml_dtypes.bfloat16).astype(np.float64), axis, -1)
    blocks = v.reshape(v.shape[:-1] + (-1, 32))
    amax = np.abs(blocks).max(-1, keepdims=True)
    byte = np.maximum(np.where(amax > 0, np.frexp(amax)[1] - 1 + 127, 0) - down, 1)
    scale = np.exp2(byte - 127.0)
    codes = (blocks / scale).astype(np.float32).astype(dtype).astype(np.float64)
    return np.moveaxis((codes * scale).reshape(v.shape), -1, axis)


WIDE = False


def mx_kscale(k):
    if not WIDE:
        return np.ones(k)
    levels = np.array([10, -10, 5, -5, 0])
    a = np.random.permutation(np.resize(levels, k // 512 * 4)).reshape(k // 512, 4)
    idx = np.arange(k)
    return np.exp2(a[idx // 512, idx % 128 // 32])


BF16 = ml_dtypes.bfloat16


def bf(x):
    return np.asarray(x, np.float32).astype(BF16)


def f64(x):
    return np.asarray(x).astype(np.float64)


B, M, N, P = 4, 2048, 1024, 128
EPS = 1e-05


def normalize(v, axes, gamma, beta):
    mean = v.mean(axis=axes, keepdims=True)
    std = np.sqrt(v.var(axis=axes, keepdims=True, ddof=1))
    return gamma * ((v - mean) / (std + EPS)) + beta


def setup_inputs():
    s = mx_kscale(N)
    return {"x": bf(np.random.standard_normal((B, M, N)) * s),
            "original_xj_y": bf(np.random.standard_normal((N, P)) * 0.5 / np.sqrt(N) / s[:, None]),
            "original_xi_y": bf(np.random.standard_normal((M, P)) * 2.0 / np.sqrt(M)),
            "gamma_o_sum": bf(1.0 + 0.1 * np.random.standard_normal(P)),
            "gamma_o": bf(1.0 + 0.1 * np.random.standard_normal((P, P))),
            "beta_o_sum": bf(0.1 * np.random.standard_normal(P)),
            "beta_o": bf(0.1 * np.random.standard_normal((P, P)))}


def reference(x, original_xj_y, original_xi_y, gamma_o_sum, gamma_o, beta_o_sum, beta_o):
    oyy = mxq(f64(x), 2, "e4m3") @ mxq(f64(original_xj_y), 0, "e4m3")
    o_sum = normalize(oyy.sum(axis=-2), (-1,), f64(gamma_o_sum), f64(beta_o_sum)) + 1.0
    oyy = mxq(np.swapaxes(oyy, -1, -2), 2, "e4m3") @ mxq(f64(original_xi_y), 0, "e4m3")
    oyy = np.swapaxes(oyy, -1, -2)
    oyy = normalize(oyy, (-2, -1), f64(gamma_o), f64(beta_o))
    return oyy, o_sum

@@ -1,0 +1,298 @@
+from contextlib import ExitStack
+
+import concourse.mybir as mybir
+from concourse.masks import make_identity
+
+F32 = mybir.dt.float32
+BF16 = mybir.dt.bfloat16
+U32 = mybir.dt.uint32
+U8 = mybir.dt.uint8
+FP8X4 = mybir.dt.float8_e4m3fn_x4
+ALU = mybir.AluOpType
+ACT = mybir.ActivationFunctionType
+
+P = 128
+PACK = 4
+K_PASS = P * PACK
+
+BATCH = 4
+ROWS = 2048
+K1 = 1024
+COLS = 128
+EPS = 1e-05
+
+PASSES_1 = K1 // K_PASS
+GROUPS_PER_BATCH = ROWS // K_PASS
+GROUPS = BATCH * GROUPS_PER_BATCH
+ROW_TILES = K_PASS // P
+WORDS = K1 // 2
+WORD_BLOCKS = WORDS // P
+QUANT_PIECES = 2
+BN_STATS = 6
+BN_AGGR = 2
+
+FLOPS = 2 * BATCH * ROWS * K1 * COLS + 2 * BATCH * COLS * ROWS * COLS
+
+
+def tile_selfprojection_pa_t_kernel(
+    tc, x, original_xj_y, original_xi_y, gamma_o_sum, gamma_o, beta_o_sum, beta_o, out_0, out_1
+):
+    nc = tc.nc
+    with ExitStack() as ctx:
+        ctx.enter_context(tc.manual_schedule())
+        const = ctx.enter_context(tc.tile_pool(name="const", bufs=1))
+        x_pool = ctx.enter_context(tc.tile_pool(name="x", bufs=GROUPS))
+        stage = ctx.enter_context(tc.tile_pool(name="stage", bufs=3))
+        y_stage = ctx.enter_context(tc.tile_pool(name="y_stage", bufs=2))
+        xt_banks = ctx.enter_context(tc.psum_pool(name="xt_banks", bufs=4))
+        y_banks = ctx.enter_context(tc.psum_pool(name="y_banks", bufs=2))
+        z_bank = ctx.enter_context(tc.psum_pool(name="z_bank", bufs=1))
+        c_bank = ctx.enter_context(tc.psum_pool(name="c_bank", bufs=1))
+
+        wj_raw = const.tile([P, PASSES_1 * PACK * COLS], BF16)
+        nc.sync.dma_start(
+            out=wj_raw[:].rearrange("p (h f) -> p h f", h=2 * PASSES_1),
+            in_=original_xj_y.rearrange("(h p e) n -> p h (e n)", h=2 * PASSES_1, p=P, e=2),
+        )
+        wi_raw = const.tile([P, GROUPS_PER_BATCH * PACK * COLS], BF16)
+        nc.sync.dma_start(
+            out=wi_raw[:].rearrange("p (g f) -> p g f", g=GROUPS_PER_BATCH),
+            in_=original_xi_y.rearrange("(g p t) n -> p g (t n)", g=GROUPS_PER_BATCH, p=P, t=PACK),
+        )
+        x_tiles = []
+        for n in range(GROUPS):
+            b, g = divmod(n, GROUPS_PER_BATCH)
+            rows = x[b].rearrange("(g p t) k -> g p (t k)", g=GROUPS_PER_BATCH, p=P, t=ROW_TILES)[g]
+            x_sb = x_pool.tile([P, ROW_TILES * K1], BF16, name="x_sb")
+            if n == 0:
+                for t in range(ROW_TILES):
+                    piece = slice(t * K1, (t + 1) * K1)
+                    nc.sync.dma_start(out=x_sb[:, piece], in_=rows[:, piece])
+            else:
+                nc.sync.dma_start(out=x_sb[:], in_=rows)
+            x_tiles.append(x_sb)
+
+        gamma_z = const.tile([P, COLS], BF16)
+        nc.scalar.dma_start(out=gamma_z[:], in_=gamma_o)
+        beta_z = const.tile([P, COLS], BF16)
+        nc.scalar.dma_start(out=beta_z[:], in_=beta_o)
+        gamma_c = const.tile([BATCH, COLS], BF16)
+        nc.scalar.dma_start(out=gamma_c[:], in_=gamma_o_sum.partition_broadcast(BATCH))
+        beta_c = const.tile([BATCH, COLS], BF16)
+        nc.scalar.dma_start(out=beta_c[:], in_=beta_o_sum.partition_broadcast(BATCH))
+
+        identity = const.tile([P, P], F32)
+        make_identity(nc, identity[:])
+        one = const.tile([P, 1], F32)
+        nc.gpsimd.memset(one[:], 1.0)
+        average = const.tile([P, P], F32)
+        nc.gpsimd.memset(average[:], 1.0 / P)
+        select = const.tile([P, BATCH, P], F32)
+        nc.gpsimd.memset(select[:], 0.0)
+        for b in range(BATCH):
+            nc.gpsimd.memset(select[:, b, b : b + 1], 1.0)
+
+        warm = const.tile([P, 1], F32)
+        nc.scalar.activation(out=warm[:], in_=one[:], func=ACT.Sqrt)
+
+        wj_grouped = const.tile([P, PASSES_1 * COLS * PACK], BF16, align_bytes=64)
+        nc.scalar.copy(
+            out=wj_grouped[:].rearrange("p (c n t) -> p c n t", c=PASSES_1, n=COLS, t=PACK),
+            in_=wj_raw[:].rearrange("p (c t n) -> p c n t", c=PASSES_1, t=PACK, n=COLS),
+        )
+        wi_grouped = const.tile([P, GROUPS_PER_BATCH * COLS * PACK], BF16, align_bytes=64)
+        nc.vector.tensor_copy(
+            out=wi_grouped[:].rearrange("p (g n t) -> p g n t", g=GROUPS_PER_BATCH, n=COLS, t=PACK),
+            in_=wi_raw[:].rearrange("p (g t n) -> p g n t", g=GROUPS_PER_BATCH, t=PACK, n=COLS),
+        )
+        wj_codes = const.tile([P, PASSES_1 * COLS], U32, align_bytes=64)
+        wj_scales = const.tile([P, PASSES_1 * COLS], U8, align_bytes=64)
+        nc.vector.quantize_mx(out=wj_codes[:].bitcast(FP8X4), scales=wj_scales[:], in_=wj_grouped[:])
+        wi_codes = const.tile([P, GROUPS_PER_BATCH * COLS], U32, align_bytes=64)
+        wi_scales = const.tile([P, GROUPS_PER_BATCH * COLS], U8, align_bytes=64)
+        nc.vector.quantize_mx(out=wi_codes[:].bitcast(FP8X4), scales=wi_scales[:], in_=wi_grouped[:])
+
+        y_codes = const.tile([P, GROUPS * COLS], U32, align_bytes=64)
+        y_scales = const.tile([P, GROUPS * COLS], U8, align_bytes=64)
+        y_sum = const.tile([P, BATCH, ROW_TILES * COLS], F32)
+        z_ps = z_bank.tile([P, BATCH, COLS], F32)
+        c_ps = c_bank.tile([P, COLS], F32)
+        z_stats = const.tile([P, BATCH, BN_STATS], F32)
+        z_mv = const.tile([P, BATCH, BN_AGGR], F32)
+
+        xt_of = {}
+        grouped_of = {}
+        codes_of = {}
+        y_of = {}
+
+        def transpose_group(n):
+            words = x_tiles[n][:].bitcast(F32)
+            xt_of[n] = []
+            for t in range(ROW_TILES):
+                xt = xt_banks.tile([P, WORD_BLOCKS * P], F32, name="xt")
+                for w in range(WORD_BLOCKS):
+                    first = t * WORDS + w * P
+                    nc.tensor.transpose(xt[:, w * P : (w + 1) * P], words[:, first : first + P], identity[:])
+                xt_of[n].append(xt)
+
+        def copy_group(n):
+            grouped = stage.tile([P, ROW_TILES * PASSES_1 * P * PACK], BF16, name="grouped", align_bytes=64)
+            pairs = grouped[:].bitcast(F32).rearrange(
+                "p (t c m u) -> p t c m u", t=ROW_TILES, c=PASSES_1, m=P, u=2
+            )
+            for t in range(ROW_TILES):
+                nc.scalar.copy(
+                    out=pairs[:, t],
+                    in_=xt_of[n][t][:].rearrange("p (c u m) -> p c m u", c=PASSES_1, u=2, m=P),
+                )
+            grouped_of[n] = grouped
+
+        def quantise_group(n):
+            width = ROW_TILES * PASSES_1 * P
+            codes = stage.tile([P, width], U32, name="codes", align_bytes=64)
+            scales = stage.tile([P, width], U8, name="scales", align_bytes=64)
+            piece = width // QUANT_PIECES
+            for h in range(QUANT_PIECES):
+                nc.vector.quantize_mx(
+                    out=codes[:, h * piece : (h + 1) * piece].bitcast(FP8X4),
+                    scales=scales[:, h * piece : (h + 1) * piece],
+                    in_=grouped_of[n][:, h * piece * PACK : (h + 1) * piece * PACK],
+                )
+            codes_of[n] = (codes, scales)
+
+        def project_group(n):
+            codes, scales = codes_of[n]
+            y_ps = y_banks.tile([P, ROW_TILES, COLS], F32, name="y_ps")
+            for t in range(ROW_TILES):
+                for c in range(PASSES_1):
+                    m_cols = slice((t * PASSES_1 + c) * P, (t * PASSES_1 + c + 1) * P)
+                    n_cols = slice(c * COLS, (c + 1) * COLS)
+                    nc.tensor.matmul_mx(
+                        out=y_ps[:, t, :],
+                        lhsT=codes[:, m_cols].bitcast(FP8X4),
+                        lhsT_scale=scales[:, m_cols],
+                        rhs=wj_codes[:, n_cols].bitcast(FP8X4),
+                        rhs_scale=wj_scales[:, n_cols],
+                        start=(c == 0),
+                        stop=(c == PASSES_1 - 1),
+                    )
+            y_of[n] = y_ps
+
+        def round_and_sum_group(n):
+            b, g = divmod(n, GROUPS_PER_BATCH)
+            y_ps = y_of[n]
+            y_grouped = y_stage.tile([P, COLS, PACK], BF16, name="y_grouped", align_bytes=64)
+            nc.vector.tensor_copy(out=y_grouped[:], in_=y_ps[:].rearrange("p t j -> p j t"))
+            flat = y_ps[:].rearrange("p t j -> p (t j)")
+            if g == 0:
+                nc.vector.tensor_copy(out=y_sum[:, b, :], in_=flat)
+            else:
+                nc.vector.tensor_tensor(out=y_sum[:, b, :], in0=flat, in1=y_sum[:, b, :], op=ALU.add)
+            cols = slice(n * COLS, (n + 1) * COLS)
+            nc.vector.quantize_mx(
+                out=y_codes[:, cols].bitcast(FP8X4),
+                scales=y_scales[:, cols],
+                in_=y_grouped[:].rearrange("p j t -> p (j t)"),
+            )
+
+        def second_contraction(n):
+            b, g = divmod(n, GROUPS_PER_BATCH)
+            i_cols = slice(g * COLS, (g + 1) * COLS)
+            j_cols = slice(n * COLS, (n + 1) * COLS)
+            nc.tensor.matmul_mx(
+                out=z_ps[:, b, :],
+                lhsT=wi_codes[:, i_cols].bitcast(FP8X4),
+                lhsT_scale=wi_scales[:, i_cols],
+                rhs=y_codes[:, j_cols].bitcast(FP8X4),
+                rhs_scale=y_scales[:, j_cols],
+                start=(g == 0),
+                stop=(g == GROUPS_PER_BATCH - 1),
+            )
+            if g == GROUPS_PER_BATCH - 1:
+                for t in range(ROW_TILES):
+                    nc.tensor.matmul(
+                        out=c_ps[:],
+                        lhsT=select[:, b, :],
+                        rhs=y_sum[:, b, t * COLS : (t + 1) * COLS],
+                        start=(b == 0 and t == 0),
+                        stop=(b == BATCH - 1 and t == ROW_TILES - 1),
+                    )
+
+        def z_row_statistics(n):
+            b, g = divmod(n, GROUPS_PER_BATCH)
+            if g == GROUPS_PER_BATCH - 1:
+                nc.vector.bn_stats(out=z_stats[:, b, :], in_=z_ps[:, b, :])
+                nc.vector.bn_aggr(out=z_mv[:, b, :], in_=z_stats[:, b, :])
+
+        def started(n):
+            return 0 <= n < GROUPS
+
+        for step in range(GROUPS + 4):
+            if started(step):
+                transpose_group(step)
+                copy_group(step)
+            if started(step - 1):
+                quantise_group(step - 1)
+                project_group(step - 1)
+            if started(step - 3):
+                second_contraction(step - 3)
+            if started(step - 2):
+                round_and_sum_group(step - 2)
+            if started(step - 4):
+                z_row_statistics(step - 4)
+
+        row_mean = z_mv[:, :, 0]
+        row_var = z_mv[:, :, 1]
+        mean_ps = xt_banks.tile([P, BATCH], F32, name="xt")
+        nc.tensor.matmul(out=mean_ps[:], lhsT=average[:], rhs=row_mean, start=True, stop=True)
+        spread = const.tile([P, BATCH], F32)
+        nc.vector.tensor_tensor(out=spread[:], in0=row_mean, in1=mean_ps[:], op=ALU.subtract)
+        nc.vector.tensor_tensor(out=spread[:], in0=spread[:], in1=spread[:], op=ALU.mult)
+        nc.vector.tensor_tensor(out=spread[:], in0=spread[:], in1=row_var, op=ALU.add)
+        var_ps = xt_banks.tile([P, BATCH], F32, name="xt")
+        nc.tensor.matmul(out=var_ps[:], lhsT=average[:], rhs=spread[:], start=True, stop=True)
+        z_mean = const.tile([P, BATCH], F32)
+        nc.vector.tensor_copy(out=z_mean[:], in_=mean_ps[:])
+
+        c_stats = const.tile([BATCH, BN_STATS], F32)
+        nc.vector.bn_stats(out=c_stats[:], in_=c_ps[:BATCH, :])
+        c_mv = const.tile([BATCH, BN_AGGR], F32)
+        nc.vector.bn_aggr(out=c_mv[:], in_=c_stats[:])
+
+        count_z = COLS * COLS
+        z_std = const.tile([P, BATCH], F32)
+        nc.scalar.activation(out=z_std[:], in_=var_ps[:], func=ACT.Sqrt, scale=count_z / (count_z - 1.0))
+        c_std = const.tile([BATCH, 1], F32)
+        nc.scalar.activation(out=c_std[:], in_=c_mv[:, 1:2], func=ACT.Sqrt, scale=COLS / (COLS - 1.0))
+
+        centred = const.tile([P, BATCH, COLS], F32)
+        for b in range(BATCH):
+            nc.vector.scalar_tensor_tensor(
+                out=centred[:, b, :], in0=z_ps[:, b, :], scalar=z_mean[:, b : b + 1], in1=gamma_z[:],
+                op0=ALU.subtract, op1=ALU.mult,
+            )
+
+        z_rstd = const.tile([P, BATCH], F32)
+        nc.vector.tensor_scalar_add(out=z_rstd[:], in0=z_std[:], scalar1=EPS)
+        nc.vector.reciprocal(out=z_rstd[:], in_=z_rstd[:])
+        z_out = const.tile([P, BATCH, COLS], F32)
+        for b in range(BATCH):
+            nc.vector.scalar_tensor_tensor(
+                out=z_out[:, b, :], in0=centred[:, b, :], scalar=z_rstd[:, b : b + 1], in1=beta_z[:],
+                op0=ALU.mult, op1=ALU.add,
+            )
+            nc.sync.dma_start(out=out_0[b], in_=z_out[:, b, :])
+
+        c_rstd = const.tile([BATCH, 1], F32)
+        nc.vector.tensor_scalar_add(out=c_rstd[:], in0=c_std[:], scalar1=EPS)
+        nc.vector.reciprocal(out=c_rstd[:], in_=c_rstd[:])
+        c_out = const.tile([BATCH, COLS], F32)
+        nc.vector.tensor_scalar(
+            out=c_out[:], in0=c_ps[:BATCH, :], scalar1=c_mv[:, 0:1], scalar2=c_rstd[:],
+            op0=ALU.subtract, op1=ALU.mult,
+        )
+        nc.vector.tensor_tensor(out=c_out[:], in0=c_out[:], in1=gamma_c[:], op=ALU.mult)
+        nc.vector.scalar_tensor_tensor(
+            out=c_out[:], in0=c_out[:], scalar=1.0, in1=beta_c[:], op0=ALU.add, op1=ALU.add
+        )
+        nc.sync.dma_start(out=out_1, in_=c_out[:])

@@ -43,11 +43,10 @@ def tile_selfprojection_pa_t_kernel(
         const = ctx.enter_context(tc.tile_pool(name="const", bufs=1))
         x_pool = ctx.enter_context(tc.tile_pool(name="x", bufs=GROUPS))
         stage = ctx.enter_context(tc.tile_pool(name="stage", bufs=3))
-        y_stage = ctx.enter_context(tc.tile_pool(name="y_stage", bufs=2))
-        xt_banks = ctx.enter_context(tc.psum_pool(name="xt_banks", bufs=4))
+        y_stage = ctx.enter_context(tc.tile_pool(name="y_stage", bufs=3))
+        xt_banks = ctx.enter_context(tc.psum_pool(name="xt_banks", bufs=5))
         y_banks = ctx.enter_context(tc.psum_pool(name="y_banks", bufs=2))
         z_bank = ctx.enter_context(tc.psum_pool(name="z_bank", bufs=1))
-        c_bank = ctx.enter_context(tc.psum_pool(name="c_bank", bufs=1))
 
         wj_raw = const.tile([P, PASSES_1 * PACK * COLS], BF16)
         nc.sync.dma_start(
@@ -92,6 +91,9 @@ def tile_selfprojection_pa_t_kernel(
         for b in range(BATCH):
             nc.gpsimd.memset(select[:, b, b : b + 1], 1.0)
 
+        beta_c_plus_1 = const.tile([BATCH, COLS], F32)
+        nc.gpsimd.tensor_scalar_add(out=beta_c_plus_1[:], in0=beta_c[:], scalar1=1.0)
+
         warm = const.tile([P, 1], F32)
         nc.scalar.activation(out=warm[:], in_=one[:], func=ACT.Sqrt)
 
@@ -116,7 +118,7 @@ def tile_selfprojection_pa_t_kernel(
         y_scales = const.tile([P, GROUPS * COLS], U8, align_bytes=64)
         y_sum = const.tile([P, BATCH, ROW_TILES * COLS], F32)
         z_ps = z_bank.tile([P, BATCH, COLS], F32)
-        c_ps = c_bank.tile([P, COLS], F32)
+        y_rows = const.tile([P, BATCH, COLS], F32)
         z_stats = const.tile([P, BATCH, BN_STATS], F32)
         z_mv = const.tile([P, BATCH, BN_AGGR], F32)
 
@@ -124,6 +126,7 @@ def tile_selfprojection_pa_t_kernel(
         grouped_of = {}
         codes_of = {}
         y_of = {}
+        y_grouped_of = {}
 
         def transpose_group(n):
             words = x_tiles[n][:].bitcast(F32)
@@ -178,21 +181,28 @@ def tile_selfprojection_pa_t_kernel(
                     )
             y_of[n] = y_ps
 
-        def round_and_sum_group(n):
-            b, g = divmod(n, GROUPS_PER_BATCH)
-            y_ps = y_of[n]
+        def scalar_rounds(n):
+            return n % 2 == 1
+
+        def round_group(n, engine_copy):
             y_grouped = y_stage.tile([P, COLS, PACK], BF16, name="y_grouped", align_bytes=64)
-            nc.vector.tensor_copy(out=y_grouped[:], in_=y_ps[:].rearrange("p t j -> p j t"))
-            flat = y_ps[:].rearrange("p t j -> p (t j)")
+            engine_copy(out=y_grouped[:], in_=y_of[n][:].rearrange("p t j -> p j t"))
+            y_grouped_of[n] = y_grouped
+
+        def sum_group(n):
+            b, g = divmod(n, GROUPS_PER_BATCH)
+            flat = y_of[n][:].rearrange("p t j -> p (t j)")
             if g == 0:
                 nc.vector.tensor_copy(out=y_sum[:, b, :], in_=flat)
             else:
                 nc.vector.tensor_tensor(out=y_sum[:, b, :], in0=flat, in1=y_sum[:, b, :], op=ALU.add)
+
+        def quantise_y_group(n):
             cols = slice(n * COLS, (n + 1) * COLS)
             nc.vector.quantize_mx(
                 out=y_codes[:, cols].bitcast(FP8X4),
                 scales=y_scales[:, cols],
-                in_=y_grouped[:].rearrange("p j t -> p (j t)"),
+                in_=y_grouped_of[n][:].rearrange("p j t -> p (j t)"),
             )
 
         def second_contraction(n):
@@ -208,21 +218,18 @@ def tile_selfprojection_pa_t_kernel(
                 start=(g == 0),
                 stop=(g == GROUPS_PER_BATCH - 1),
             )
-            if g == GROUPS_PER_BATCH - 1:
-                for t in range(ROW_TILES):
-                    nc.tensor.matmul(
-                        out=c_ps[:],
-                        lhsT=select[:, b, :],
-                        rhs=y_sum[:, b, t * COLS : (t + 1) * COLS],
-                        start=(b == 0 and t == 0),
-                        stop=(b == BATCH - 1 and t == ROW_TILES - 1),
-                    )
 
-        def z_row_statistics(n):
+        def batch_statistics(n):
             b, g = divmod(n, GROUPS_PER_BATCH)
             if g == GROUPS_PER_BATCH - 1:
                 nc.vector.bn_stats(out=z_stats[:, b, :], in_=z_ps[:, b, :])
                 nc.vector.bn_aggr(out=z_mv[:, b, :], in_=z_stats[:, b, :])
+                nc.vector.tensor_reduce(
+                    out=y_rows[:, b, :],
+                    in_=y_sum[:, b, :].rearrange("p (t j) -> p j t", t=ROW_TILES),
+                    axis=mybir.AxisListType.X,
+                    op=ALU.add,
+                )
 
         def started(n):
             return 0 <= n < GROUPS
@@ -230,47 +237,65 @@ def tile_selfprojection_pa_t_kernel(
         for step in range(GROUPS + 4):
             if started(step):
                 transpose_group(step)
-                copy_group(step)
             if started(step - 1):
                 quantise_group(step - 1)
                 project_group(step - 1)
             if started(step - 3):
                 second_contraction(step - 3)
+            if started(step):
+                copy_group(step)
+            if started(step - 1) and scalar_rounds(step - 1):
+                round_group(step - 1, nc.scalar.copy)
             if started(step - 2):
-                round_and_sum_group(step - 2)
+                if scalar_rounds(step - 2):
+                    quantise_y_group(step - 2)
+                    sum_group(step - 2)
+                else:
+                    round_group(step - 2, nc.vector.tensor_copy)
+                    sum_group(step - 2)
+                    quantise_y_group(step - 2)
             if started(step - 4):
-                z_row_statistics(step - 4)
+                batch_statistics(step - 4)
 
         row_mean = z_mv[:, :, 0]
         row_var = z_mv[:, :, 1]
         mean_ps = xt_banks.tile([P, BATCH], F32, name="xt")
         nc.tensor.matmul(out=mean_ps[:], lhsT=average[:], rhs=row_mean, start=True, stop=True)
+        c_ps = xt_banks.tile([P, COLS], F32, name="xt")
+        for b in range(BATCH):
+            nc.tensor.matmul(
+                out=c_ps[:], lhsT=select[:, b, :], rhs=y_rows[:, b, :], start=(b == 0), stop=(b == BATCH - 1)
+            )
         spread = const.tile([P, BATCH], F32)
         nc.vector.tensor_tensor(out=spread[:], in0=row_mean, in1=mean_ps[:], op=ALU.subtract)
         nc.vector.tensor_tensor(out=spread[:], in0=spread[:], in1=spread[:], op=ALU.mult)
         nc.vector.tensor_tensor(out=spread[:], in0=spread[:], in1=row_var, op=ALU.add)
         var_ps = xt_banks.tile([P, BATCH], F32, name="xt")
         nc.tensor.matmul(out=var_ps[:], lhsT=average[:], rhs=spread[:], start=True, stop=True)
-        z_mean = const.tile([P, BATCH], F32)
-        nc.vector.tensor_copy(out=z_mean[:], in_=mean_ps[:])
-
-        c_stats = const.tile([BATCH, BN_STATS], F32)
-        nc.vector.bn_stats(out=c_stats[:], in_=c_ps[:BATCH, :])
-        c_mv = const.tile([BATCH, BN_AGGR], F32)
-        nc.vector.bn_aggr(out=c_mv[:], in_=c_stats[:])
-
         count_z = COLS * COLS
         z_std = const.tile([P, BATCH], F32)
         nc.scalar.activation(out=z_std[:], in_=var_ps[:], func=ACT.Sqrt, scale=count_z / (count_z - 1.0))
-        c_std = const.tile([BATCH, 1], F32)
-        nc.scalar.activation(out=c_std[:], in_=c_mv[:, 1:2], func=ACT.Sqrt, scale=COLS / (COLS - 1.0))
 
+        z_mean = const.tile([P, BATCH], F32)
+        nc.vector.tensor_copy(out=z_mean[:], in_=mean_ps[:])
         centred = const.tile([P, BATCH, COLS], F32)
         for b in range(BATCH):
             nc.vector.scalar_tensor_tensor(
                 out=centred[:, b, :], in0=z_ps[:, b, :], scalar=z_mean[:, b : b + 1], in1=gamma_z[:],
                 op0=ALU.subtract, op1=ALU.mult,
             )
+
+        c_stats = const.tile([BATCH, BN_STATS], F32)
+        nc.vector.bn_stats(out=c_stats[:], in_=c_ps[:BATCH, :])
+        c_mv = const.tile([BATCH, BN_AGGR], F32)
+        nc.vector.bn_aggr(out=c_mv[:], in_=c_stats[:])
+        c_std = const.tile([BATCH, 1], F32)
+        nc.scalar.activation(out=c_std[:], in_=c_mv[:, 1:2], func=ACT.Sqrt, scale=COLS / (COLS - 1.0))
+        c_centred = const.tile([BATCH, COLS], F32)
+        nc.vector.scalar_tensor_tensor(
+            out=c_centred[:], in0=c_ps[:BATCH, :], scalar=c_mv[:, 0:1], in1=gamma_c[:],
+            op0=ALU.subtract, op1=ALU.mult,
+        )
 
         z_rstd = const.tile([P, BATCH], F32)
         nc.vector.tensor_scalar_add(out=z_rstd[:], in0=z_std[:], scalar1=EPS)
@@ -287,12 +312,7 @@ def tile_selfprojection_pa_t_kernel(
         nc.vector.tensor_scalar_add(out=c_rstd[:], in0=c_std[:], scalar1=EPS)
         nc.vector.reciprocal(out=c_rstd[:], in_=c_rstd[:])
         c_out = const.tile([BATCH, COLS], F32)
-        nc.vector.tensor_scalar(
-            out=c_out[:], in0=c_ps[:BATCH, :], scalar1=c_mv[:, 0:1], scalar2=c_rstd[:],
-            op0=ALU.subtract, op1=ALU.mult,
-        )
-        nc.vector.tensor_tensor(out=c_out[:], in0=c_out[:], in1=gamma_c[:], op=ALU.mult)
         nc.vector.scalar_tensor_tensor(
-            out=c_out[:], in0=c_out[:], scalar=1.0, in1=beta_c[:], op0=ALU.add, op1=ALU.add
+            out=c_out[:], in0=c_centred[:], scalar=c_rstd[:], in1=beta_c_plus_1[:], op0=ALU.mult, op1=ALU.add
         )
         nc.sync.dma_start(out=out_1, in_=c_out[:])

@@ -28,6 +28,7 @@ ROW_TILES = K_PASS // P
 WORDS = K1 // 2
 WORD_BLOCKS = WORDS // P
 QUANT_PIECES = 2
+WARM_GROUPS = 2
 BN_STATS = 6
 BN_AGGR = 2
 
@@ -44,9 +45,10 @@ def tile_selfprojection_pa_t_kernel(
         x_pool = ctx.enter_context(tc.tile_pool(name="x", bufs=GROUPS))
         stage = ctx.enter_context(tc.tile_pool(name="stage", bufs=3))
         y_stage = ctx.enter_context(tc.tile_pool(name="y_stage", bufs=3))
-        xt_banks = ctx.enter_context(tc.psum_pool(name="xt_banks", bufs=5))
+        xt_banks = ctx.enter_context(tc.psum_pool(name="xt_banks", bufs=4))
         y_banks = ctx.enter_context(tc.psum_pool(name="y_banks", bufs=2))
         z_bank = ctx.enter_context(tc.psum_pool(name="z_bank", bufs=1))
+        c_bank = ctx.enter_context(tc.psum_pool(name="c_bank", bufs=1))
 
         wj_raw = const.tile([P, PASSES_1 * PACK * COLS], BF16)
         nc.sync.dma_start(
@@ -91,6 +93,8 @@ def tile_selfprojection_pa_t_kernel(
         for b in range(BATCH):
             nc.gpsimd.memset(select[:, b, b : b + 1], 1.0)
 
+        zeros = const.tile([P, ROW_TILES * COLS], BF16)
+        nc.gpsimd.memset(zeros[:], 0.0)
         beta_c_plus_1 = const.tile([BATCH, COLS], F32)
         nc.gpsimd.tensor_scalar_add(out=beta_c_plus_1[:], in0=beta_c[:], scalar1=1.0)
 
@@ -116,9 +120,9 @@ def tile_selfprojection_pa_t_kernel(
 
         y_codes = const.tile([P, GROUPS * COLS], U32, align_bytes=64)
         y_scales = const.tile([P, GROUPS * COLS], U8, align_bytes=64)
-        y_sum = const.tile([P, BATCH, ROW_TILES * COLS], F32)
         z_ps = z_bank.tile([P, BATCH, COLS], F32)
-        y_rows = const.tile([P, BATCH, COLS], F32)
+        c_whole_bank = c_bank.tile([P, ROW_TILES * COLS], F32)
+        c_ps = c_whole_bank[:, :COLS]
         z_stats = const.tile([P, BATCH, BN_STATS], F32)
         z_mv = const.tile([P, BATCH, BN_AGGR], F32)
 
@@ -127,6 +131,7 @@ def tile_selfprojection_pa_t_kernel(
         codes_of = {}
         y_of = {}
         y_grouped_of = {}
+        y_rows_of = {}
 
         def transpose_group(n):
             words = x_tiles[n][:].bitcast(F32)
@@ -137,6 +142,8 @@ def tile_selfprojection_pa_t_kernel(
                     first = t * WORDS + w * P
                     nc.tensor.transpose(xt[:, w * P : (w + 1) * P], words[:, first : first + P], identity[:])
                 xt_of[n].append(xt)
+                if n < WARM_GROUPS:
+                    nc.tensor.matmul(out=c_whole_bank[:], lhsT=zeros[:, :P], rhs=zeros[:], start=True, stop=True)
 
         def copy_group(n):
             grouped = stage.tile([P, ROW_TILES * PASSES_1 * P * PACK], BF16, name="grouped", align_bytes=64)
@@ -190,12 +197,11 @@ def tile_selfprojection_pa_t_kernel(
             y_grouped_of[n] = y_grouped
 
         def sum_group(n):
-            b, g = divmod(n, GROUPS_PER_BATCH)
-            flat = y_of[n][:].rearrange("p t j -> p (t j)")
-            if g == 0:
-                nc.vector.tensor_copy(out=y_sum[:, b, :], in_=flat)
-            else:
-                nc.vector.tensor_tensor(out=y_sum[:, b, :], in0=flat, in1=y_sum[:, b, :], op=ALU.add)
+            y_rows = y_stage.tile([P, COLS], F32, name="y_rows")
+            nc.vector.tensor_reduce(
+                out=y_rows[:], in_=y_of[n][:].rearrange("p t j -> p j t"), axis=mybir.AxisListType.X, op=ALU.add
+            )
+            y_rows_of[n] = y_rows
 
         def quantise_y_group(n):
             cols = slice(n * COLS, (n + 1) * COLS)
@@ -218,18 +224,15 @@ def tile_selfprojection_pa_t_kernel(
                 start=(g == 0),
                 stop=(g == GROUPS_PER_BATCH - 1),
             )
+            nc.tensor.matmul(
+                out=c_ps, lhsT=select[:, b, :], rhs=y_rows_of[n][:], start=(n == 0), stop=(n == GROUPS - 1)
+            )
 
         def batch_statistics(n):
             b, g = divmod(n, GROUPS_PER_BATCH)
             if g == GROUPS_PER_BATCH - 1:
                 nc.vector.bn_stats(out=z_stats[:, b, :], in_=z_ps[:, b, :])
                 nc.vector.bn_aggr(out=z_mv[:, b, :], in_=z_stats[:, b, :])
-                nc.vector.tensor_reduce(
-                    out=y_rows[:, b, :],
-                    in_=y_sum[:, b, :].rearrange("p (t j) -> p j t", t=ROW_TILES),
-                    axis=mybir.AxisListType.X,
-                    op=ALU.add,
-                )
 
         def started(n):
             return 0 <= n < GROUPS
@@ -261,11 +264,6 @@ def tile_selfprojection_pa_t_kernel(
         row_var = z_mv[:, :, 1]
         mean_ps = xt_banks.tile([P, BATCH], F32, name="xt")
         nc.tensor.matmul(out=mean_ps[:], lhsT=average[:], rhs=row_mean, start=True, stop=True)
-        c_ps = xt_banks.tile([P, COLS], F32, name="xt")
-        for b in range(BATCH):
-            nc.tensor.matmul(
-                out=c_ps[:], lhsT=select[:, b, :], rhs=y_rows[:, b, :], start=(b == 0), stop=(b == BATCH - 1)
-            )
         spread = const.tile([P, BATCH], F32)
         nc.vector.tensor_tensor(out=spread[:], in0=row_mean, in1=mean_ps[:], op=ALU.subtract)
         nc.vector.tensor_tensor(out=spread[:], in0=spread[:], in1=spread[:], op=ALU.mult)

@@ -27,10 +27,12 @@ GROUPS = BATCH * GROUPS_PER_BATCH
 ROW_TILES = K_PASS // P
 WORDS = K1 // 2
 WORD_BLOCKS = WORDS // P
-QUANT_PIECES = 2
 WARM_GROUPS = 2
 BN_STATS = 6
 BN_AGGR = 2
+PAIRS = 2
+PAIR_COLS = ROW_TILES // PAIRS * P
+Y_WORDS = K_PASS // 2
 
 FLOPS = 2 * BATCH * ROWS * K1 * COLS + 2 * BATCH * COLS * ROWS * COLS
 
@@ -47,8 +49,8 @@ def tile_selfprojection_pa_t_kernel(
         y_stage = ctx.enter_context(tc.tile_pool(name="y_stage", bufs=3))
         xt_banks = ctx.enter_context(tc.psum_pool(name="xt_banks", bufs=4))
         y_banks = ctx.enter_context(tc.psum_pool(name="y_banks", bufs=2))
+        yw_banks = ctx.enter_context(tc.psum_pool(name="yw_banks", bufs=1))
         z_bank = ctx.enter_context(tc.psum_pool(name="z_bank", bufs=1))
-        c_bank = ctx.enter_context(tc.psum_pool(name="c_bank", bufs=1))
 
         wj_raw = const.tile([P, PASSES_1 * PACK * COLS], BF16)
         nc.sync.dma_start(
@@ -88,10 +90,8 @@ def tile_selfprojection_pa_t_kernel(
         nc.gpsimd.memset(one[:], 1.0)
         average = const.tile([P, P], F32)
         nc.gpsimd.memset(average[:], 1.0 / P)
-        select = const.tile([P, BATCH, P], F32)
-        nc.gpsimd.memset(select[:], 0.0)
-        for b in range(BATCH):
-            nc.gpsimd.memset(select[:, b, b : b + 1], 1.0)
+        c_columns = const.tile([P, P], F32)
+        nc.gpsimd.memset(c_columns[:], 0.0)
 
         zeros = const.tile([P, ROW_TILES * COLS], BF16)
         nc.gpsimd.memset(zeros[:], 0.0)
@@ -121,8 +121,7 @@ def tile_selfprojection_pa_t_kernel(
         y_codes = const.tile([P, GROUPS * COLS], U32, align_bytes=64)
         y_scales = const.tile([P, GROUPS * COLS], U8, align_bytes=64)
         z_ps = z_bank.tile([P, BATCH, COLS], F32)
-        c_whole_bank = c_bank.tile([P, ROW_TILES * COLS], F32)
-        c_ps = c_whole_bank[:, :COLS]
+        c_parts = const.tile([P, BATCH, GROUPS_PER_BATCH], F32)
         z_stats = const.tile([P, BATCH, BN_STATS], F32)
         z_mv = const.tile([P, BATCH, BN_AGGR], F32)
 
@@ -130,85 +129,98 @@ def tile_selfprojection_pa_t_kernel(
         grouped_of = {}
         codes_of = {}
         y_of = {}
+        y_rounded_of = {}
+        y_words_of = {}
         y_grouped_of = {}
-        y_rows_of = {}
+        warm_bank = yw_banks.tile([P, ROW_TILES * COLS], F32, name="yw")
 
         def transpose_group(n):
             words = x_tiles[n][:].bitcast(F32)
-            xt_of[n] = []
-            for t in range(ROW_TILES):
-                xt = xt_banks.tile([P, WORD_BLOCKS * P], F32, name="xt")
-                for w in range(WORD_BLOCKS):
-                    first = t * WORDS + w * P
-                    nc.tensor.transpose(xt[:, w * P : (w + 1) * P], words[:, first : first + P], identity[:])
-                xt_of[n].append(xt)
-                if n < WARM_GROUPS:
-                    nc.tensor.matmul(out=c_whole_bank[:], lhsT=zeros[:, :P], rhs=zeros[:], start=True, stop=True)
+            for u in range(PAIRS):
+                for c in range(PASSES_1):
+                    xt = xt_banks.tile([P, WORD_BLOCKS * P], F32, name="xt")
+                    for e in range(ROW_TILES // PAIRS):
+                        for w in range(WORD_BLOCKS // PASSES_1):
+                            first = (2 * u + e) * WORDS + (2 * c + w) * P
+                            slot = 2 * e + w
+                            nc.tensor.transpose(
+                                xt[:, slot * P : (slot + 1) * P], words[:, first : first + P], identity[:]
+                            )
+                    xt_of[n, u, c] = xt
+                    if n < WARM_GROUPS:
+                        nc.tensor.matmul(out=warm_bank[:], lhsT=zeros[:, :P], rhs=zeros[:], start=True, stop=True)
 
-        def copy_group(n):
-            grouped = stage.tile([P, ROW_TILES * PASSES_1 * P * PACK], BF16, name="grouped", align_bytes=64)
-            pairs = grouped[:].bitcast(F32).rearrange(
-                "p (t c m u) -> p t c m u", t=ROW_TILES, c=PASSES_1, m=P, u=2
+        def copy_bank(n, u, c, engine_copy):
+            if (u, c) == (0, 0):
+                grouped_of[n] = stage.tile(
+                    [P, PAIRS * PASSES_1 * PAIR_COLS * PACK], BF16, name="grouped", align_bytes=64
+                )
+            pairs = grouped_of[n][:].bitcast(F32).rearrange(
+                "p (u c m s) -> p u c m s", u=PAIRS, c=PASSES_1, m=P, s=WORD_BLOCKS
             )
-            for t in range(ROW_TILES):
-                nc.scalar.copy(
-                    out=pairs[:, t],
-                    in_=xt_of[n][t][:].rearrange("p (c u m) -> p c m u", c=PASSES_1, u=2, m=P),
-                )
-            grouped_of[n] = grouped
+            engine_copy(out=pairs[:, u, c], in_=xt_of[n, u, c][:].rearrange("p (s m) -> p m s", s=WORD_BLOCKS))
 
-        def quantise_group(n):
-            width = ROW_TILES * PASSES_1 * P
-            codes = stage.tile([P, width], U32, name="codes", align_bytes=64)
-            scales = stage.tile([P, width], U8, name="scales", align_bytes=64)
-            piece = width // QUANT_PIECES
-            for h in range(QUANT_PIECES):
-                nc.vector.quantize_mx(
-                    out=codes[:, h * piece : (h + 1) * piece].bitcast(FP8X4),
-                    scales=scales[:, h * piece : (h + 1) * piece],
-                    in_=grouped_of[n][:, h * piece * PACK : (h + 1) * piece * PACK],
+        def quantise_pair(n, u):
+            width = PASSES_1 * PAIR_COLS
+            if u == 0:
+                codes_of[n] = (
+                    stage.tile([P, PAIRS * width], U32, name="codes", align_bytes=64),
+                    stage.tile([P, PAIRS * width], U8, name="scales", align_bytes=64),
                 )
-            codes_of[n] = (codes, scales)
+            codes, scales = codes_of[n]
+            cols = slice(u * width, (u + 1) * width)
+            nc.vector.quantize_mx(
+                out=codes[:, cols].bitcast(FP8X4),
+                scales=scales[:, cols],
+                in_=grouped_of[n][:, u * width * PACK : (u + 1) * width * PACK],
+            )
 
         def project_group(n):
             codes, scales = codes_of[n]
-            y_ps = y_banks.tile([P, ROW_TILES, COLS], F32, name="y_ps")
-            for t in range(ROW_TILES):
+            y_ps = y_banks.tile([P, PAIRS * PAIR_COLS], F32, name="y_ps")
+            for u in range(PAIRS):
                 for c in range(PASSES_1):
-                    m_cols = slice((t * PASSES_1 + c) * P, (t * PASSES_1 + c + 1) * P)
+                    first = (u * PASSES_1 + c) * PAIR_COLS
+                    m_cols = slice(first, first + PAIR_COLS)
                     n_cols = slice(c * COLS, (c + 1) * COLS)
                     nc.tensor.matmul_mx(
-                        out=y_ps[:, t, :],
-                        lhsT=codes[:, m_cols].bitcast(FP8X4),
-                        lhsT_scale=scales[:, m_cols],
-                        rhs=wj_codes[:, n_cols].bitcast(FP8X4),
-                        rhs_scale=wj_scales[:, n_cols],
+                        out=y_ps[:, u * PAIR_COLS : (u + 1) * PAIR_COLS],
+                        lhsT=wj_codes[:, n_cols].bitcast(FP8X4),
+                        lhsT_scale=wj_scales[:, n_cols],
+                        rhs=codes[:, m_cols].bitcast(FP8X4),
+                        rhs_scale=scales[:, m_cols],
                         start=(c == 0),
                         stop=(c == PASSES_1 - 1),
                     )
             y_of[n] = y_ps
 
-        def scalar_rounds(n):
-            return n % 2 == 1
-
-        def round_group(n, engine_copy):
-            y_grouped = y_stage.tile([P, COLS, PACK], BF16, name="y_grouped", align_bytes=64)
-            engine_copy(out=y_grouped[:], in_=y_of[n][:].rearrange("p t j -> p j t"))
-            y_grouped_of[n] = y_grouped
-
-        def sum_group(n):
-            y_rows = y_stage.tile([P, COLS], F32, name="y_rows")
-            nc.vector.tensor_reduce(
-                out=y_rows[:], in_=y_of[n][:].rearrange("p t j -> p j t"), axis=mybir.AxisListType.X, op=ALU.add
+        def round_group(n):
+            b, g = divmod(n, GROUPS_PER_BATCH)
+            y_rounded = y_stage.tile([P, K_PASS], BF16, name="y_rounded", align_bytes=64)
+            nc.scalar.activation(
+                out=y_rounded[:], in_=y_of[n][:], func=ACT.Copy, accum_out=c_parts[:, b, g : g + 1]
             )
-            y_rows_of[n] = y_rows
+            y_rounded_of[n] = y_rounded
+
+        def transpose_y_group(n):
+            y_words = yw_banks.tile([P, PAIRS, COLS], F32, name="yw")
+            words = y_rounded_of[n][:].bitcast(F32)
+            for u in range(PAIRS):
+                nc.tensor.transpose(y_words[:, u, :], words[:, u * P : (u + 1) * P], identity[:])
+            y_words_of[n] = y_words
+
+        def copy_y_group(n):
+            y_grouped = y_stage.tile([P, COLS * PACK], BF16, name="y_grouped", align_bytes=64)
+            nc.vector.tensor_copy(
+                out=y_grouped[:].bitcast(F32).rearrange("p (j u) -> p j u", u=PAIRS),
+                in_=y_words_of[n][:].rearrange("p u j -> p j u"),
+            )
+            y_grouped_of[n] = y_grouped
 
         def quantise_y_group(n):
             cols = slice(n * COLS, (n + 1) * COLS)
             nc.vector.quantize_mx(
-                out=y_codes[:, cols].bitcast(FP8X4),
-                scales=y_scales[:, cols],
-                in_=y_grouped_of[n][:].rearrange("p j t -> p (j t)"),
+                out=y_codes[:, cols].bitcast(FP8X4), scales=y_scales[:, cols], in_=y_grouped_of[n][:]
             )
 
         def second_contraction(n):
@@ -224,9 +236,6 @@ def tile_selfprojection_pa_t_kernel(
                 start=(g == 0),
                 stop=(g == GROUPS_PER_BATCH - 1),
             )
-            nc.tensor.matmul(
-                out=c_ps, lhsT=select[:, b, :], rhs=y_rows_of[n][:], start=(n == 0), stop=(n == GROUPS - 1)
-            )
 
         def batch_statistics(n):
             b, g = divmod(n, GROUPS_PER_BATCH)
@@ -238,25 +247,28 @@ def tile_selfprojection_pa_t_kernel(
             return 0 <= n < GROUPS
 
         for step in range(GROUPS + 4):
+            if started(step - 2):
+                transpose_y_group(step - 2)
             if started(step):
                 transpose_group(step)
             if started(step - 1):
-                quantise_group(step - 1)
+                for u in range(PAIRS):
+                    quantise_pair(step - 1, u)
                 project_group(step - 1)
+            if started(step - 2):
+                copy_y_group(step - 2)
             if started(step - 3):
                 second_contraction(step - 3)
             if started(step):
-                copy_group(step)
-            if started(step - 1) and scalar_rounds(step - 1):
-                round_group(step - 1, nc.scalar.copy)
+                copy_bank(step, 0, 0, nc.scalar.copy)
+                copy_bank(step, 0, 1, nc.scalar.copy)
+            if started(step - 1):
+                round_group(step - 1)
+            if started(step):
+                copy_bank(step, 1, 0, nc.scalar.copy)
+                copy_bank(step, 1, 1, nc.vector.tensor_copy)
             if started(step - 2):
-                if scalar_rounds(step - 2):
-                    quantise_y_group(step - 2)
-                    sum_group(step - 2)
-                else:
-                    round_group(step - 2, nc.vector.tensor_copy)
-                    sum_group(step - 2)
-                    quantise_y_group(step - 2)
+                quantise_y_group(step - 2)
             if started(step - 4):
                 batch_statistics(step - 4)
 
@@ -283,6 +295,9 @@ def tile_selfprojection_pa_t_kernel(
                 op0=ALU.subtract, op1=ALU.mult,
             )
 
+        nc.vector.tensor_reduce(out=c_columns[:, :BATCH], in_=c_parts[:], axis=mybir.AxisListType.X, op=ALU.add)
+        c_ps = xt_banks.tile([P, P], F32, name="xt")
+        nc.tensor.transpose(c_ps[:], c_columns[:], identity[:])
         c_stats = const.tile([BATCH, BN_STATS], F32)
         nc.vector.bn_stats(out=c_stats[:], in_=c_ps[:BATCH, :])
         c_mv = const.tile([BATCH, BN_AGGR], F32)

@@ -47,8 +47,8 @@ def tile_selfprojection_pa_t_kernel(
         x_pool = ctx.enter_context(tc.tile_pool(name="x", bufs=GROUPS))
         stage = ctx.enter_context(tc.tile_pool(name="stage", bufs=3))
         y_stage = ctx.enter_context(tc.tile_pool(name="y_stage", bufs=3))
-        xt_banks = ctx.enter_context(tc.psum_pool(name="xt_banks", bufs=4))
-        y_banks = ctx.enter_context(tc.psum_pool(name="y_banks", bufs=2))
+        xt_banks = ctx.enter_context(tc.psum_pool(name="xt_banks", bufs=5))
+        y_banks = ctx.enter_context(tc.psum_pool(name="y_banks", bufs=1))
         yw_banks = ctx.enter_context(tc.psum_pool(name="yw_banks", bufs=1))
         z_bank = ctx.enter_context(tc.psum_pool(name="z_bank", bufs=1))
 
@@ -247,28 +247,26 @@ def tile_selfprojection_pa_t_kernel(
             return 0 <= n < GROUPS
 
         for step in range(GROUPS + 4):
-            if started(step - 2):
-                transpose_y_group(step - 2)
             if started(step):
                 transpose_group(step)
+            if started(step - 2):
+                transpose_y_group(step - 2)
             if started(step - 1):
                 for u in range(PAIRS):
                     quantise_pair(step - 1, u)
                 project_group(step - 1)
-            if started(step - 2):
-                copy_y_group(step - 2)
             if started(step - 3):
+                quantise_y_group(step - 3)
                 second_contraction(step - 3)
             if started(step):
                 copy_bank(step, 0, 0, nc.scalar.copy)
                 copy_bank(step, 0, 1, nc.scalar.copy)
-            if started(step - 1):
-                round_group(step - 1)
-            if started(step):
                 copy_bank(step, 1, 0, nc.scalar.copy)
                 copy_bank(step, 1, 1, nc.vector.tensor_copy)
+            if started(step - 1):
+                round_group(step - 1)
             if started(step - 2):
-                quantise_y_group(step - 2)
+                copy_y_group(step - 2)
             if started(step - 4):
                 batch_statistics(step - 4)
 

@@ -27,6 +27,7 @@ GROUPS = BATCH * GROUPS_PER_BATCH
 ROW_TILES = K_PASS // P
 WORDS = K1 // 2
 WORD_BLOCKS = WORDS // P
+WARM_START = 5
 WARM_GROUPS = 2
 BN_STATS = 6
 BN_AGGR = 2
@@ -53,27 +54,47 @@ def tile_selfprojection_pa_t_kernel(
         z_bank = ctx.enter_context(tc.psum_pool(name="z_bank", bufs=1))
 
         wj_raw = const.tile([P, PASSES_1 * PACK * COLS], BF16)
-        nc.sync.dma_start(
-            out=wj_raw[:].rearrange("p (h f) -> p h f", h=2 * PASSES_1),
-            in_=original_xj_y.rearrange("(h p e) n -> p h (e n)", h=2 * PASSES_1, p=P, e=2),
-        )
         wi_raw = const.tile([P, GROUPS_PER_BATCH * PACK * COLS], BF16)
-        nc.sync.dma_start(
-            out=wi_raw[:].rearrange("p (g f) -> p g f", g=GROUPS_PER_BATCH),
-            in_=original_xi_y.rearrange("(g p t) n -> p g (t n)", g=GROUPS_PER_BATCH, p=P, t=PACK),
-        )
+
+        def load_wj():
+            nc.sync.dma_start(
+                out=wj_raw[:].rearrange("p (h f) -> p h f", h=2 * PASSES_1),
+                in_=original_xj_y.rearrange("(h p e) n -> p h (e n)", h=2 * PASSES_1, p=P, e=2),
+            )
+
+        def load_wi():
+            nc.sync.dma_start(
+                out=wi_raw[:].rearrange("p (g f) -> p g f", g=GROUPS_PER_BATCH),
+                in_=original_xi_y.rearrange("(g p t) n -> p g (t n)", g=GROUPS_PER_BATCH, p=P, t=PACK),
+            )
+
         x_tiles = []
-        for n in range(GROUPS):
+
+        def load_x(n, first_tile, tiles, first_col, cols):
             b, g = divmod(n, GROUPS_PER_BATCH)
-            rows = x[b].rearrange("(g p t) k -> g p (t k)", g=GROUPS_PER_BATCH, p=P, t=ROW_TILES)[g]
+            rows = x[b].rearrange("(g p t) k -> g p t k", g=GROUPS_PER_BATCH, p=P, t=ROW_TILES)[g]
+            t = slice(first_tile, first_tile + tiles)
+            k = slice(first_col, first_col + cols)
+            nc.sync.dma_start(
+                out=x_tiles[n][:].rearrange("p (t k) -> p t k", t=ROW_TILES)[:, t, k], in_=rows[:, t, k]
+            )
+
+        def load_x_halves(n):
+            for u in range(PAIRS):
+                load_x(n, 2 * u, 2, 0, K1)
+
+        for n in range(GROUPS):
             x_sb = x_pool.tile([P, ROW_TILES * K1], BF16, name="x_sb")
-            if n == 0:
-                for t in range(ROW_TILES):
-                    piece = slice(t * K1, (t + 1) * K1)
-                    nc.sync.dma_start(out=x_sb[:, piece], in_=rows[:, piece])
-            else:
-                nc.sync.dma_start(out=x_sb[:], in_=rows)
             x_tiles.append(x_sb)
+        load_x(0, 0, 2, 0, K_PASS)
+        load_x(0, 0, 2, K_PASS, K_PASS)
+        load_wj()
+        load_x(0, 2, 2, 0, K1)
+        load_wi()
+        load_x_halves(1)
+        for n in range(2, GROUPS - 1):
+            load_x(n, 0, ROW_TILES, 0, K1)
+        load_x_halves(GROUPS - 1)
 
         gamma_z = const.tile([P, COLS], BF16)
         nc.scalar.dma_start(out=gamma_z[:], in_=gamma_o)
@@ -84,17 +105,18 @@ def tile_selfprojection_pa_t_kernel(
         beta_c = const.tile([BATCH, COLS], BF16)
         nc.scalar.dma_start(out=beta_c[:], in_=beta_o_sum.partition_broadcast(BATCH))
 
+        zeros = const.tile([P, ROW_TILES * COLS], BF16)
+        nc.gpsimd.memset(zeros[:], 0.0)
         identity = const.tile([P, P], F32)
         make_identity(nc, identity[:])
         one = const.tile([P, 1], F32)
         nc.gpsimd.memset(one[:], 1.0)
         average = const.tile([P, P], F32)
         nc.gpsimd.memset(average[:], 1.0 / P)
+        centre = const.tile([P, P], F32)
+        nc.gpsimd.tensor_tensor(out=centre[:], in0=identity[:], in1=average[:], op=ALU.subtract)
         c_columns = const.tile([P, P], F32)
         nc.gpsimd.memset(c_columns[:], 0.0)
-
-        zeros = const.tile([P, ROW_TILES * COLS], BF16)
-        nc.gpsimd.memset(zeros[:], 0.0)
         beta_c_plus_1 = const.tile([BATCH, COLS], F32)
         nc.gpsimd.tensor_scalar_add(out=beta_c_plus_1[:], in0=beta_c[:], scalar1=1.0)
 
@@ -102,26 +124,24 @@ def tile_selfprojection_pa_t_kernel(
         nc.scalar.activation(out=warm[:], in_=one[:], func=ACT.Sqrt)
 
         wj_grouped = const.tile([P, PASSES_1 * COLS * PACK], BF16, align_bytes=64)
-        nc.scalar.copy(
-            out=wj_grouped[:].rearrange("p (c n t) -> p c n t", c=PASSES_1, n=COLS, t=PACK),
-            in_=wj_raw[:].rearrange("p (c t n) -> p c n t", c=PASSES_1, t=PACK, n=COLS),
-        )
-        wi_grouped = const.tile([P, GROUPS_PER_BATCH * COLS * PACK], BF16, align_bytes=64)
-        nc.vector.tensor_copy(
-            out=wi_grouped[:].rearrange("p (g n t) -> p g n t", g=GROUPS_PER_BATCH, n=COLS, t=PACK),
-            in_=wi_raw[:].rearrange("p (g t n) -> p g n t", g=GROUPS_PER_BATCH, t=PACK, n=COLS),
-        )
         wj_codes = const.tile([P, PASSES_1 * COLS], U32, align_bytes=64)
         wj_scales = const.tile([P, PASSES_1 * COLS], U8, align_bytes=64)
-        nc.vector.quantize_mx(out=wj_codes[:].bitcast(FP8X4), scales=wj_scales[:], in_=wj_grouped[:])
+        wi_grouped = const.tile([P, GROUPS_PER_BATCH * COLS * PACK], BF16, align_bytes=64)
         wi_codes = const.tile([P, GROUPS_PER_BATCH * COLS], U32, align_bytes=64)
         wi_scales = const.tile([P, GROUPS_PER_BATCH * COLS], U8, align_bytes=64)
-        nc.vector.quantize_mx(out=wi_codes[:].bitcast(FP8X4), scales=wi_scales[:], in_=wi_grouped[:])
+
+        def quantise_weight(raw, grouped, codes, scales, blocks):
+            nc.vector.tensor_copy(
+                out=grouped[:].rearrange("p (c n t) -> p c n t", c=blocks, n=COLS, t=PACK),
+                in_=raw[:].rearrange("p (c t n) -> p c n t", c=blocks, t=PACK, n=COLS),
+            )
+            nc.vector.quantize_mx(out=codes[:].bitcast(FP8X4), scales=scales[:], in_=grouped[:])
 
         y_codes = const.tile([P, GROUPS * COLS], U32, align_bytes=64)
         y_scales = const.tile([P, GROUPS * COLS], U8, align_bytes=64)
         z_ps = z_bank.tile([P, BATCH, COLS], F32)
-        c_parts = const.tile([P, BATCH, GROUPS_PER_BATCH], F32)
+        c_parts = const.tile([P, BATCH, GROUPS_PER_BATCH + 1], F32)
+        nc.gpsimd.memset(c_parts[:], 0.0)
         z_stats = const.tile([P, BATCH, BN_STATS], F32)
         z_mv = const.tile([P, BATCH, BN_AGGR], F32)
 
@@ -133,6 +153,9 @@ def tile_selfprojection_pa_t_kernel(
         y_words_of = {}
         y_grouped_of = {}
         warm_bank = yw_banks.tile([P, ROW_TILES * COLS], F32, name="yw")
+
+        def keep_warm():
+            nc.tensor.matmul(out=warm_bank[:], lhsT=zeros[:, :P], rhs=zeros[:], start=True, stop=True)
 
         def transpose_group(n):
             words = x_tiles[n][:].bitcast(F32)
@@ -148,7 +171,7 @@ def tile_selfprojection_pa_t_kernel(
                             )
                     xt_of[n, u, c] = xt
                     if n < WARM_GROUPS:
-                        nc.tensor.matmul(out=warm_bank[:], lhsT=zeros[:, :P], rhs=zeros[:], start=True, stop=True)
+                        keep_warm()
 
         def copy_bank(n, u, c, engine_copy):
             if (u, c) == (0, 0):
@@ -178,13 +201,19 @@ def tile_selfprojection_pa_t_kernel(
         def project_group(n):
             codes, scales = codes_of[n]
             y_ps = y_banks.tile([P, PAIRS * PAIR_COLS], F32, name="y_ps")
+            y_of[n] = [y_ps[:, u * PAIR_COLS : (u + 1) * PAIR_COLS] for u in range(PAIRS)]
+            if n == GROUPS - 1:
+                last_y_ps = xt_banks.tile([P, PAIR_COLS], F32, name="xt")
+                y_of[n][PAIRS - 1] = last_y_ps[:]
+            else:
+                y_of[n].append(y_ps)
             for u in range(PAIRS):
                 for c in range(PASSES_1):
                     first = (u * PASSES_1 + c) * PAIR_COLS
                     m_cols = slice(first, first + PAIR_COLS)
                     n_cols = slice(c * COLS, (c + 1) * COLS)
                     nc.tensor.matmul_mx(
-                        out=y_ps[:, u * PAIR_COLS : (u + 1) * PAIR_COLS],
+                        out=y_of[n][u],
                         lhsT=wj_codes[:, n_cols].bitcast(FP8X4),
                         lhsT_scale=wj_scales[:, n_cols],
                         rhs=codes[:, m_cols].bitcast(FP8X4),
@@ -192,26 +221,37 @@ def tile_selfprojection_pa_t_kernel(
                         start=(c == 0),
                         stop=(c == PASSES_1 - 1),
                     )
-            y_of[n] = y_ps
 
         def round_group(n):
             b, g = divmod(n, GROUPS_PER_BATCH)
             y_rounded = y_stage.tile([P, K_PASS], BF16, name="y_rounded", align_bytes=64)
-            nc.scalar.activation(
-                out=y_rounded[:], in_=y_of[n][:], func=ACT.Copy, accum_out=c_parts[:, b, g : g + 1]
-            )
+            if n == GROUPS - 1:
+                for u in range(PAIRS):
+                    nc.scalar.activation(
+                        out=y_rounded[:, u * PAIR_COLS : (u + 1) * PAIR_COLS],
+                        in_=y_of[n][u],
+                        func=ACT.Copy,
+                        accum_out=c_parts[:, b, g + u : g + u + 1],
+                    )
+            else:
+                nc.scalar.activation(
+                    out=y_rounded[:], in_=y_of[n][PAIRS][:], func=ACT.Copy, accum_out=c_parts[:, b, g : g + 1]
+                )
             y_rounded_of[n] = y_rounded
 
         def transpose_y_group(n):
-            y_words = yw_banks.tile([P, PAIRS, COLS], F32, name="yw")
+            if n < GROUPS - 2:
+                y_words = yw_banks.tile([P, PAIRS, COLS], F32, name="yw")
+            else:
+                y_words = xt_banks.tile([P, PAIRS, COLS], F32, name="xt")
             words = y_rounded_of[n][:].bitcast(F32)
             for u in range(PAIRS):
                 nc.tensor.transpose(y_words[:, u, :], words[:, u * P : (u + 1) * P], identity[:])
             y_words_of[n] = y_words
 
-        def copy_y_group(n):
+        def copy_y_group(n, engine_copy):
             y_grouped = y_stage.tile([P, COLS * PACK], BF16, name="y_grouped", align_bytes=64)
-            nc.vector.tensor_copy(
+            engine_copy(
                 out=y_grouped[:].bitcast(F32).rearrange("p (j u) -> p j u", u=PAIRS),
                 in_=y_words_of[n][:].rearrange("p u j -> p j u"),
             )
@@ -237,93 +277,172 @@ def tile_selfprojection_pa_t_kernel(
                 stop=(g == GROUPS_PER_BATCH - 1),
             )
 
-        def batch_statistics(n):
-            b, g = divmod(n, GROUPS_PER_BATCH)
-            if g == GROUPS_PER_BATCH - 1:
-                nc.vector.bn_stats(out=z_stats[:, b, :], in_=z_ps[:, b, :])
-                nc.vector.bn_aggr(out=z_mv[:, b, :], in_=z_stats[:, b, :])
+        count_z = COLS * COLS
+        z_dev = const.tile([P, BATCH], F32)
+        z_spread = const.tile([P, BATCH], F32)
+        z_std = const.tile([P, BATCH], F32)
+        z_rstd = const.tile([P, BATCH], F32)
+        centred = const.tile([P, BATCH, COLS], F32)
+        z_out = const.tile([P, BATCH, COLS], F32)
+        dev_of = {}
+        mean_of = {}
+        var_of = {}
+
+        def z_row_moments(b):
+            nc.vector.bn_stats(out=z_stats[:, b, :], in_=z_ps[:, b, :])
+            nc.vector.bn_aggr(out=z_mv[:, b, :], in_=z_stats[:, b, :])
+
+        def z_mean(lo, hi):
+            row_mean = z_mv[:, lo:hi, 0]
+            moments = xt_banks.tile([P, 2, hi - lo], F32, name="xt")
+            nc.tensor.matmul(out=moments[:, 0, :], lhsT=centre[:], rhs=row_mean, start=True, stop=True)
+            nc.tensor.matmul(out=moments[:, 1, :], lhsT=average[:], rhs=row_mean, start=True, stop=True)
+            dev_of[lo] = moments[:, 0, :]
+            for b in range(lo, hi):
+                mean_of[b] = moments[:, 1, b - lo : b - lo + 1]
+
+        def z_spread_one(b):
+            nc.vector.scalar_tensor_tensor(
+                out=z_spread[:, b : b + 1], in0=dev_of[b], scalar=dev_of[b], in1=z_mv[:, b, 1:2],
+                op0=ALU.mult, op1=ALU.add,
+            )
+
+        def z_spread_several(lo, hi):
+            cols = slice(lo, hi)
+            nc.vector.tensor_copy(out=z_dev[:, cols], in_=dev_of[lo])
+            nc.vector.tensor_tensor(out=z_spread[:, cols], in0=z_dev[:, cols], in1=z_dev[:, cols], op=ALU.mult)
+            nc.vector.tensor_tensor(
+                out=z_spread[:, cols], in0=z_spread[:, cols], in1=z_mv[:, lo:hi, 1], op=ALU.add
+            )
+
+        def z_centre(b):
+            nc.vector.scalar_tensor_tensor(
+                out=centred[:, b, :], in0=z_ps[:, b, :], scalar=mean_of[b], in1=gamma_z[:],
+                op0=ALU.subtract, op1=ALU.mult,
+            )
+
+        def z_variance(lo, hi):
+            cols = slice(lo, hi)
+            var_ps = xt_banks.tile([P, hi - lo], F32, name="xt")
+            nc.tensor.matmul(out=var_ps[:], lhsT=average[:], rhs=z_spread[:, cols], start=True, stop=True)
+            nc.scalar.activation(
+                out=z_std[:, cols], in_=var_ps[:], func=ACT.Sqrt, scale=count_z / (count_z - 1.0)
+            )
+
+        def z_reciprocal(lo, hi):
+            cols = slice(lo, hi)
+            nc.vector.tensor_scalar_add(out=z_rstd[:, cols], in0=z_std[:, cols], scalar1=EPS)
+            nc.vector.reciprocal(out=z_rstd[:, cols], in_=z_rstd[:, cols])
+
+        def z_scale(b):
+            nc.vector.scalar_tensor_tensor(
+                out=z_out[:, b, :], in0=centred[:, b, :], scalar=z_rstd[:, b : b + 1], in1=beta_z[:],
+                op0=ALU.mult, op1=ALU.add,
+            )
+
+        def z_store(lo, hi):
+            nc.sync.dma_start(out=out_0[lo:hi].rearrange("b p n -> p b n"), in_=z_out[:, lo:hi, :])
+
+        c_stats = const.tile([BATCH, BN_STATS], F32)
+        c_mv = const.tile([BATCH, BN_AGGR], F32)
+        c_std = const.tile([BATCH, 1], F32)
+        c_rstd = const.tile([BATCH, 1], F32)
+        c_centred = const.tile([BATCH, COLS], F32)
+        c_out = const.tile([BATCH, COLS], F32)
+        c_rows_of = {}
+
+        def c_to_rows():
+            nc.vector.tensor_reduce(out=c_columns[:, :BATCH], in_=c_parts[:], axis=mybir.AxisListType.X, op=ALU.add)
+            c_ps = xt_banks.tile([P, P], F32, name="xt")
+            nc.tensor.transpose(c_ps[:], c_columns[:], identity[:])
+            c_rows_of[0] = c_ps
+
+        def c_moments():
+            nc.vector.bn_stats(out=c_stats[:], in_=c_rows_of[0][:BATCH, :])
+            nc.vector.bn_aggr(out=c_mv[:], in_=c_stats[:])
+            nc.scalar.activation(out=c_std[:], in_=c_mv[:, 1:2], func=ACT.Sqrt, scale=COLS / (COLS - 1.0))
+
+        def c_store():
+            nc.vector.scalar_tensor_tensor(
+                out=c_centred[:], in0=c_rows_of[0][:BATCH, :], scalar=c_mv[:, 0:1], in1=gamma_c[:],
+                op0=ALU.subtract, op1=ALU.mult,
+            )
+            nc.vector.tensor_scalar_add(out=c_rstd[:], in0=c_std[:], scalar1=EPS)
+            nc.vector.reciprocal(out=c_rstd[:], in_=c_rstd[:])
+            nc.vector.scalar_tensor_tensor(
+                out=c_out[:], in0=c_centred[:], scalar=c_rstd[:], in1=beta_c_plus_1[:], op0=ALU.mult, op1=ALU.add
+            )
+            nc.sync.dma_start(out=out_1, in_=c_out[:])
 
         def started(n):
             return 0 <= n < GROUPS
 
-        for step in range(GROUPS + 4):
-            if started(step):
-                transpose_group(step)
+        def batch_ending(n):
+            return n // GROUPS_PER_BATCH if started(n) and n % GROUPS_PER_BATCH == GROUPS_PER_BATCH - 1 else None
+
+        last = BATCH - 1
+        for i in range(WARM_START):
+            keep_warm()
+        quantise_weight(wj_raw, wj_grouped, wj_codes, wj_scales, PASSES_1)
+        for step in range(GROUPS):
+            transpose_group(step)
             if started(step - 2):
                 transpose_y_group(step - 2)
             if started(step - 1):
                 for u in range(PAIRS):
                     quantise_pair(step - 1, u)
                 project_group(step - 1)
-            if started(step - 3):
+            if step == 1:
+                quantise_weight(wi_raw, wi_grouped, wi_codes, wi_scales, GROUPS_PER_BATCH)
+            if started(step - 3) and step < GROUPS - 1:
                 quantise_y_group(step - 3)
                 second_contraction(step - 3)
-            if started(step):
-                copy_bank(step, 0, 0, nc.scalar.copy)
-                copy_bank(step, 0, 1, nc.scalar.copy)
-                copy_bank(step, 1, 0, nc.scalar.copy)
-                copy_bank(step, 1, 1, nc.vector.tensor_copy)
+            copy_bank(step, 0, 0, nc.scalar.copy)
+            copy_bank(step, 0, 1, nc.scalar.copy)
+            copy_bank(step, 1, 0, nc.vector.tensor_copy)
+            copy_bank(step, 1, 1, nc.scalar.copy)
             if started(step - 1):
                 round_group(step - 1)
-            if started(step - 2):
-                copy_y_group(step - 2)
-            if started(step - 4):
-                batch_statistics(step - 4)
+            if started(step - 2) and step < GROUPS - 1:
+                copy_y_group(step - 2, nc.scalar.copy if step % 4 == 1 else nc.vector.tensor_copy)
+            if batch_ending(step - 4) is not None and step < GROUPS - 1:
+                z_row_moments(batch_ending(step - 4))
 
-        row_mean = z_mv[:, :, 0]
-        row_var = z_mv[:, :, 1]
-        mean_ps = xt_banks.tile([P, BATCH], F32, name="xt")
-        nc.tensor.matmul(out=mean_ps[:], lhsT=average[:], rhs=row_mean, start=True, stop=True)
-        spread = const.tile([P, BATCH], F32)
-        nc.vector.tensor_tensor(out=spread[:], in0=row_mean, in1=mean_ps[:], op=ALU.subtract)
-        nc.vector.tensor_tensor(out=spread[:], in0=spread[:], in1=spread[:], op=ALU.mult)
-        nc.vector.tensor_tensor(out=spread[:], in0=spread[:], in1=row_var, op=ALU.add)
-        var_ps = xt_banks.tile([P, BATCH], F32, name="xt")
-        nc.tensor.matmul(out=var_ps[:], lhsT=average[:], rhs=spread[:], start=True, stop=True)
-        count_z = COLS * COLS
-        z_std = const.tile([P, BATCH], F32)
-        nc.scalar.activation(out=z_std[:], in_=var_ps[:], func=ACT.Sqrt, scale=count_z / (count_z - 1.0))
+        end = GROUPS - 1
+        for u in range(PAIRS):
+            quantise_pair(end, u)
+        project_group(end)
+        round_group(end)
+        transpose_y_group(end - 1)
+        transpose_y_group(end)
+        quantise_y_group(end - 3)
+        copy_y_group(end - 2, nc.vector.tensor_copy)
+        quantise_y_group(end - 2)
+        copy_y_group(end - 1, nc.vector.tensor_copy)
+        z_row_moments(last - 1)
+        copy_y_group(end, nc.vector.tensor_copy)
+        quantise_y_group(end - 1)
+        quantise_y_group(end)
+        z_mean(0, last)
+        for n in range(end - 3, end + 1):
+            second_contraction(n)
+        c_to_rows()
+        z_spread_several(0, last)
+        z_variance(0, last)
 
-        z_mean = const.tile([P, BATCH], F32)
-        nc.vector.tensor_copy(out=z_mean[:], in_=mean_ps[:])
-        centred = const.tile([P, BATCH, COLS], F32)
-        for b in range(BATCH):
-            nc.vector.scalar_tensor_tensor(
-                out=centred[:, b, :], in0=z_ps[:, b, :], scalar=z_mean[:, b : b + 1], in1=gamma_z[:],
-                op0=ALU.subtract, op1=ALU.mult,
-            )
-
-        nc.vector.tensor_reduce(out=c_columns[:, :BATCH], in_=c_parts[:], axis=mybir.AxisListType.X, op=ALU.add)
-        c_ps = xt_banks.tile([P, P], F32, name="xt")
-        nc.tensor.transpose(c_ps[:], c_columns[:], identity[:])
-        c_stats = const.tile([BATCH, BN_STATS], F32)
-        nc.vector.bn_stats(out=c_stats[:], in_=c_ps[:BATCH, :])
-        c_mv = const.tile([BATCH, BN_AGGR], F32)
-        nc.vector.bn_aggr(out=c_mv[:], in_=c_stats[:])
-        c_std = const.tile([BATCH, 1], F32)
-        nc.scalar.activation(out=c_std[:], in_=c_mv[:, 1:2], func=ACT.Sqrt, scale=COLS / (COLS - 1.0))
-        c_centred = const.tile([BATCH, COLS], F32)
-        nc.vector.scalar_tensor_tensor(
-            out=c_centred[:], in0=c_ps[:BATCH, :], scalar=c_mv[:, 0:1], in1=gamma_c[:],
-            op0=ALU.subtract, op1=ALU.mult,
-        )
-
-        z_rstd = const.tile([P, BATCH], F32)
-        nc.vector.tensor_scalar_add(out=z_rstd[:], in0=z_std[:], scalar1=EPS)
-        nc.vector.reciprocal(out=z_rstd[:], in_=z_rstd[:])
-        z_out = const.tile([P, BATCH, COLS], F32)
-        for b in range(BATCH):
-            nc.vector.scalar_tensor_tensor(
-                out=z_out[:, b, :], in0=centred[:, b, :], scalar=z_rstd[:, b : b + 1], in1=beta_z[:],
-                op0=ALU.mult, op1=ALU.add,
-            )
-            nc.sync.dma_start(out=out_0[b], in_=z_out[:, b, :])
-
-        c_rstd = const.tile([BATCH, 1], F32)
-        nc.vector.tensor_scalar_add(out=c_rstd[:], in0=c_std[:], scalar1=EPS)
-        nc.vector.reciprocal(out=c_rstd[:], in_=c_rstd[:])
-        c_out = const.tile([BATCH, COLS], F32)
-        nc.vector.scalar_tensor_tensor(
-            out=c_out[:], in0=c_centred[:], scalar=c_rstd[:], in1=beta_c_plus_1[:], op0=ALU.mult, op1=ALU.add
-        )
-        nc.sync.dma_start(out=out_1, in_=c_out[:])
+        z_row_moments(last)
+        z_mean(last, BATCH)
+        for b in range(last):
+            z_centre(b)
+        z_spread_one(last)
+        z_variance(last, BATCH)
+        c_moments()
+        z_centre(last)
+        z_reciprocal(0, last)
+        for b in range(last):
+            z_scale(b)
+        z_store(0, last)
+        c_store()
+        z_reciprocal(last, BATCH)
+        z_scale(last)
+        z_store(last, BATCH)

@@ -139,9 +139,9 @@ def tile_selfprojection_pa_t_kernel(
 
         y_codes = const.tile([P, GROUPS * COLS], U32, align_bytes=64)
         y_scales = const.tile([P, GROUPS * COLS], U8, align_bytes=64)
-        z_ps = z_bank.tile([P, BATCH, COLS], F32)
-        c_parts = const.tile([P, BATCH, GROUPS_PER_BATCH + 1], F32)
-        nc.gpsimd.memset(c_parts[:], 0.0)
+        z_ps = z_bank.tile([P, BATCH - 1, COLS], F32)
+        z_of = [z_ps[:, b, :] for b in range(BATCH - 1)]
+        c_parts = const.tile([P, BATCH, GROUPS_PER_BATCH], F32)
         z_stats = const.tile([P, BATCH, BN_STATS], F32)
         z_mv = const.tile([P, BATCH, BN_AGGR], F32)
 
@@ -178,10 +178,19 @@ def tile_selfprojection_pa_t_kernel(
                 grouped_of[n] = stage.tile(
                     [P, PAIRS * PASSES_1 * PAIR_COLS * PACK], BF16, name="grouped", align_bytes=64
                 )
-            pairs = grouped_of[n][:].bitcast(F32).rearrange(
-                "p (u c m s) -> p u c m s", u=PAIRS, c=PASSES_1, m=P, s=WORD_BLOCKS
-            )
-            engine_copy(out=pairs[:, u, c], in_=xt_of[n, u, c][:].rearrange("p (s m) -> p m s", s=WORD_BLOCKS))
+            words = grouped_of[n][:].bitcast(F32)
+            bank = slice((u * PASSES_1 + c) * WORD_BLOCKS * P, (u * PASSES_1 + c + 1) * WORD_BLOCKS * P)
+            xt = xt_of[n, u, c][:]
+            if n == GROUPS - 1:
+                engine_copy(
+                    out=words[:, bank].rearrange("p (e m w) -> p e m w", e=2, m=P, w=2),
+                    in_=xt.rearrange("p (e w m) -> p e m w", e=2, w=2, m=P),
+                )
+            else:
+                engine_copy(
+                    out=words[:, bank].rearrange("p (m s) -> p m s", m=P, s=WORD_BLOCKS),
+                    in_=xt.rearrange("p (s m) -> p m s", s=WORD_BLOCKS, m=P),
+                )
 
         def quantise_pair(n, u):
             width = PASSES_1 * PAIR_COLS
@@ -198,46 +207,69 @@ def tile_selfprojection_pa_t_kernel(
                 in_=grouped_of[n][:, u * width * PACK : (u + 1) * width * PACK],
             )
 
+        def project(out, lhsT, lhsT_scale, rhs, rhs_scale, first, last_pass):
+            nc.tensor.matmul_mx(
+                out=out, lhsT=lhsT.bitcast(FP8X4), lhsT_scale=lhsT_scale, rhs=rhs.bitcast(FP8X4),
+                rhs_scale=rhs_scale, start=first, stop=last_pass,
+            )
+
         def project_group(n):
             codes, scales = codes_of[n]
             y_ps = y_banks.tile([P, PAIRS * PAIR_COLS], F32, name="y_ps")
-            y_of[n] = [y_ps[:, u * PAIR_COLS : (u + 1) * PAIR_COLS] for u in range(PAIRS)]
-            if n == GROUPS - 1:
-                last_y_ps = xt_banks.tile([P, PAIR_COLS], F32, name="xt")
-                y_of[n][PAIRS - 1] = last_y_ps[:]
-            else:
-                y_of[n].append(y_ps)
+            y_of[n] = y_ps
             for u in range(PAIRS):
                 for c in range(PASSES_1):
                     first = (u * PASSES_1 + c) * PAIR_COLS
                     m_cols = slice(first, first + PAIR_COLS)
                     n_cols = slice(c * COLS, (c + 1) * COLS)
-                    nc.tensor.matmul_mx(
-                        out=y_of[n][u],
-                        lhsT=wj_codes[:, n_cols].bitcast(FP8X4),
-                        lhsT_scale=wj_scales[:, n_cols],
-                        rhs=codes[:, m_cols].bitcast(FP8X4),
-                        rhs_scale=scales[:, m_cols],
-                        start=(c == 0),
-                        stop=(c == PASSES_1 - 1),
+                    project(
+                        y_ps[:, u * PAIR_COLS : (u + 1) * PAIR_COLS], wj_codes[:, n_cols], wj_scales[:, n_cols],
+                        codes[:, m_cols], scales[:, m_cols], c == 0, c == PASSES_1 - 1,
                     )
 
         def round_group(n):
             b, g = divmod(n, GROUPS_PER_BATCH)
             y_rounded = y_stage.tile([P, K_PASS], BF16, name="y_rounded", align_bytes=64)
-            if n == GROUPS - 1:
-                for u in range(PAIRS):
-                    nc.scalar.activation(
-                        out=y_rounded[:, u * PAIR_COLS : (u + 1) * PAIR_COLS],
-                        in_=y_of[n][u],
-                        func=ACT.Copy,
-                        accum_out=c_parts[:, b, g + u : g + u + 1],
-                    )
-            else:
-                nc.scalar.activation(
-                    out=y_rounded[:], in_=y_of[n][PAIRS][:], func=ACT.Copy, accum_out=c_parts[:, b, g : g + 1]
-                )
+            nc.scalar.activation(
+                out=y_rounded[:], in_=y_of[n][:], func=ACT.Copy, accum_out=c_parts[:, b, g : g + 1]
+            )
             y_rounded_of[n] = y_rounded
+
+        def project_last_pair(n, u):
+            codes, scales = codes_of[n]
+            y_ps = xt_banks.tile([P, ROW_TILES // PAIRS, COLS], F32, name="xt")
+            for e in range(ROW_TILES // PAIRS):
+                for c in range(PASSES_1):
+                    first = ((u * PASSES_1 + c) * 2 + e) * P
+                    m_cols = slice(first, first + P)
+                    n_cols = slice(c * COLS, (c + 1) * COLS)
+                    project(
+                        y_ps[:, e, :], codes[:, m_cols], scales[:, m_cols], wj_codes[:, n_cols],
+                        wj_scales[:, n_cols], c == 0, c == PASSES_1 - 1,
+                    )
+            return y_ps
+
+        def round_last_pair(n, u, y_ps):
+            if u == 0:
+                y_grouped_of[n] = y_stage.tile([P, COLS * PACK], BF16, name="y_grouped", align_bytes=64)
+            tiles = y_grouped_of[n][:].rearrange("p (j u e) -> p u j e", j=COLS, u=PAIRS, e=2)
+            nc.scalar.copy(out=tiles[:, u], in_=y_ps[:].rearrange("p e j -> p j e"))
+
+        def sum_last_group(n):
+            b, g = divmod(n, GROUPS_PER_BATCH)
+            codes, scales = codes_of[n]
+            y_ps = y_banks.tile([P, PAIR_COLS], F32, name="y_ps")
+            passes = [(u, c) for u in range(PAIRS) for c in range(PASSES_1)]
+            for u, c in passes:
+                first = (u * PASSES_1 + c) * PAIR_COLS
+                m_cols = slice(first, first + PAIR_COLS)
+                n_cols = slice(c * COLS, (c + 1) * COLS)
+                project(
+                    y_ps[:], wj_codes[:, n_cols], wj_scales[:, n_cols], codes[:, m_cols], scales[:, m_cols],
+                    (u, c) == passes[0], (u, c) == passes[-1],
+                )
+            sums = y_stage.tile([P, PAIR_COLS], F32, name="sums")
+            nc.scalar.activation(out=sums[:], in_=y_ps[:], func=ACT.Copy, accum_out=c_parts[:, b, g : g + 1])
 
         def transpose_y_group(n):
             if n < GROUPS - 2:
@@ -268,7 +300,7 @@ def tile_selfprojection_pa_t_kernel(
             i_cols = slice(g * COLS, (g + 1) * COLS)
             j_cols = slice(n * COLS, (n + 1) * COLS)
             nc.tensor.matmul_mx(
-                out=z_ps[:, b, :],
+                out=z_of[b],
                 lhsT=wi_codes[:, i_cols].bitcast(FP8X4),
                 lhsT_scale=wi_scales[:, i_cols],
                 rhs=y_codes[:, j_cols].bitcast(FP8X4),
@@ -277,8 +309,8 @@ def tile_selfprojection_pa_t_kernel(
                 stop=(g == GROUPS_PER_BATCH - 1),
             )
 
+        last = BATCH - 1
         count_z = COLS * COLS
-        z_dev = const.tile([P, BATCH], F32)
         z_spread = const.tile([P, BATCH], F32)
         z_std = const.tile([P, BATCH], F32)
         z_rstd = const.tile([P, BATCH], F32)
@@ -289,35 +321,28 @@ def tile_selfprojection_pa_t_kernel(
         var_of = {}
 
         def z_row_moments(b):
-            nc.vector.bn_stats(out=z_stats[:, b, :], in_=z_ps[:, b, :])
+            nc.vector.bn_stats(out=z_stats[:, b, :], in_=z_of[b])
             nc.vector.bn_aggr(out=z_mv[:, b, :], in_=z_stats[:, b, :])
 
         def z_mean(lo, hi):
             row_mean = z_mv[:, lo:hi, 0]
-            moments = xt_banks.tile([P, 2, hi - lo], F32, name="xt")
-            nc.tensor.matmul(out=moments[:, 0, :], lhsT=centre[:], rhs=row_mean, start=True, stop=True)
-            nc.tensor.matmul(out=moments[:, 1, :], lhsT=average[:], rhs=row_mean, start=True, stop=True)
-            dev_of[lo] = moments[:, 0, :]
+            dev_ps = xt_banks.tile([P, hi - lo], F32, name="xt")
+            nc.tensor.matmul(out=dev_ps[:], lhsT=centre[:], rhs=row_mean, start=True, stop=True)
+            mean_ps = xt_banks.tile([P, hi - lo], F32, name="xt")
+            nc.tensor.matmul(out=mean_ps[:], lhsT=average[:], rhs=row_mean, start=True, stop=True)
             for b in range(lo, hi):
-                mean_of[b] = moments[:, 1, b - lo : b - lo + 1]
+                dev_of[b] = dev_ps[:, b - lo : b - lo + 1]
+                mean_of[b] = mean_ps[:, b - lo : b - lo + 1]
 
-        def z_spread_one(b):
+        def z_spread_of(b):
             nc.vector.scalar_tensor_tensor(
                 out=z_spread[:, b : b + 1], in0=dev_of[b], scalar=dev_of[b], in1=z_mv[:, b, 1:2],
                 op0=ALU.mult, op1=ALU.add,
             )
 
-        def z_spread_several(lo, hi):
-            cols = slice(lo, hi)
-            nc.vector.tensor_copy(out=z_dev[:, cols], in_=dev_of[lo])
-            nc.vector.tensor_tensor(out=z_spread[:, cols], in0=z_dev[:, cols], in1=z_dev[:, cols], op=ALU.mult)
-            nc.vector.tensor_tensor(
-                out=z_spread[:, cols], in0=z_spread[:, cols], in1=z_mv[:, lo:hi, 1], op=ALU.add
-            )
-
         def z_centre(b):
             nc.vector.scalar_tensor_tensor(
-                out=centred[:, b, :], in0=z_ps[:, b, :], scalar=mean_of[b], in1=gamma_z[:],
+                out=centred[:, b, :], in0=z_of[b], scalar=mean_of[b], in1=gamma_z[:],
                 op0=ALU.subtract, op1=ALU.mult,
             )
 
@@ -353,26 +378,32 @@ def tile_selfprojection_pa_t_kernel(
 
         def c_to_rows():
             nc.vector.tensor_reduce(out=c_columns[:, :BATCH], in_=c_parts[:], axis=mybir.AxisListType.X, op=ALU.add)
-            c_ps = xt_banks.tile([P, P], F32, name="xt")
+            c_ps = y_banks.tile([P, P], F32, name="y_ps")
             nc.tensor.transpose(c_ps[:], c_columns[:], identity[:])
             c_rows_of[0] = c_ps
 
-        def c_moments():
+        def c_row_moments():
             nc.vector.bn_stats(out=c_stats[:], in_=c_rows_of[0][:BATCH, :])
+
+        def c_moments():
             nc.vector.bn_aggr(out=c_mv[:], in_=c_stats[:])
             nc.scalar.activation(out=c_std[:], in_=c_mv[:, 1:2], func=ACT.Sqrt, scale=COLS / (COLS - 1.0))
 
-        def c_store():
+        def c_centre():
             nc.vector.scalar_tensor_tensor(
                 out=c_centred[:], in0=c_rows_of[0][:BATCH, :], scalar=c_mv[:, 0:1], in1=gamma_c[:],
                 op0=ALU.subtract, op1=ALU.mult,
             )
+
+        def c_reciprocal():
             nc.vector.tensor_scalar_add(out=c_rstd[:], in0=c_std[:], scalar1=EPS)
             nc.vector.reciprocal(out=c_rstd[:], in_=c_rstd[:])
+
+        def c_store():
             nc.vector.scalar_tensor_tensor(
                 out=c_out[:], in0=c_centred[:], scalar=c_rstd[:], in1=beta_c_plus_1[:], op0=ALU.mult, op1=ALU.add
             )
-            nc.sync.dma_start(out=out_1, in_=c_out[:])
+            nc.scalar.dma_start(out=out_1, in_=c_out[:])
 
         def started(n):
             return 0 <= n < GROUPS
@@ -380,7 +411,6 @@ def tile_selfprojection_pa_t_kernel(
         def batch_ending(n):
             return n // GROUPS_PER_BATCH if started(n) and n % GROUPS_PER_BATCH == GROUPS_PER_BATCH - 1 else None
 
-        last = BATCH - 1
         for i in range(WARM_START):
             keep_warm()
         quantise_weight(wj_raw, wj_grouped, wj_codes, wj_scales, PASSES_1)
@@ -404,45 +434,55 @@ def tile_selfprojection_pa_t_kernel(
             if started(step - 1):
                 round_group(step - 1)
             if started(step - 2) and step < GROUPS - 1:
-                copy_y_group(step - 2, nc.scalar.copy if step % 4 == 1 else nc.vector.tensor_copy)
+                copy_y_group(step - 2, nc.vector.tensor_copy)
             if batch_ending(step - 4) is not None and step < GROUPS - 1:
                 z_row_moments(batch_ending(step - 4))
 
         end = GROUPS - 1
-        for u in range(PAIRS):
-            quantise_pair(end, u)
-        project_group(end)
-        round_group(end)
+        half = BATCH // 2
+        z_mean(0, half)
+        quantise_pair(end, 0)
+        y_first = project_last_pair(end, 0)
+        quantise_pair(end, 1)
         transpose_y_group(end - 1)
-        transpose_y_group(end)
+        y_second = project_last_pair(end, 1)
+        copy_y_group(end - 2, nc.scalar.copy)
+        round_last_pair(end, 0, y_first)
+        copy_y_group(end - 1, nc.scalar.copy)
+        round_last_pair(end, 1, y_second)
         quantise_y_group(end - 3)
-        copy_y_group(end - 2, nc.vector.tensor_copy)
         quantise_y_group(end - 2)
-        copy_y_group(end - 1, nc.vector.tensor_copy)
-        z_row_moments(last - 1)
-        copy_y_group(end, nc.vector.tensor_copy)
+        for b in range(half):
+            z_spread_of(b)
         quantise_y_group(end - 1)
+        z_variance(0, half)
+        sum_last_group(end)
+        z_row_moments(last - 1)
         quantise_y_group(end)
-        z_mean(0, last)
+        z_last = yw_banks.tile([P, COLS], F32, name="yw")
+        z_of.append(z_last[:])
         for n in range(end - 3, end + 1):
             second_contraction(n)
-        c_to_rows()
-        z_spread_several(0, last)
-        z_variance(0, last)
-
-        z_row_moments(last)
-        z_mean(last, BATCH)
-        for b in range(last):
+        for b in range(half):
             z_centre(b)
-        z_spread_one(last)
-        z_variance(last, BATCH)
-        c_moments()
-        z_centre(last)
-        z_reciprocal(0, last)
-        for b in range(last):
+        c_to_rows()
+        z_row_moments(last)
+        z_mean(half, BATCH)
+        z_reciprocal(0, half)
+        for b in range(half):
             z_scale(b)
-        z_store(0, last)
+        z_store(0, half)
+        c_row_moments()
+        for b in range(half, BATCH):
+            z_spread_of(b)
+        c_moments()
+        z_variance(half, BATCH)
+        for b in range(half, BATCH):
+            z_centre(b)
+        c_centre()
+        z_reciprocal(half, BATCH)
+        for b in range(half, BATCH):
+            z_scale(b)
+        z_store(half, BATCH)
+        c_reciprocal()
         c_store()
-        z_reciprocal(last, BATCH)
-        z_scale(last)
-        z_store(last, BATCH)

@@ -27,8 +27,9 @@ GROUPS = BATCH * GROUPS_PER_BATCH
 ROW_TILES = K_PASS // P
 WORDS = K1 // 2
 WORD_BLOCKS = WORDS // P
+HALF_LOADS = 3
 WARM_START = 5
-WARM_GROUPS = 2
+WARM_GROUPS = 1
 BN_STATS = 6
 BN_AGGR = 2
 PAIRS = 2
@@ -48,9 +49,8 @@ def tile_selfprojection_pa_t_kernel(
         x_pool = ctx.enter_context(tc.tile_pool(name="x", bufs=GROUPS))
         stage = ctx.enter_context(tc.tile_pool(name="stage", bufs=3))
         y_stage = ctx.enter_context(tc.tile_pool(name="y_stage", bufs=3))
-        xt_banks = ctx.enter_context(tc.psum_pool(name="xt_banks", bufs=5))
+        xt_banks = ctx.enter_context(tc.psum_pool(name="xt_banks", bufs=6))
         y_banks = ctx.enter_context(tc.psum_pool(name="y_banks", bufs=1))
-        yw_banks = ctx.enter_context(tc.psum_pool(name="yw_banks", bufs=1))
         z_bank = ctx.enter_context(tc.psum_pool(name="z_bank", bufs=1))
 
         wj_raw = const.tile([P, PASSES_1 * PACK * COLS], BF16)
@@ -91,10 +91,11 @@ def tile_selfprojection_pa_t_kernel(
         load_wj()
         load_x(0, 2, 2, 0, K1)
         load_wi()
-        load_x_halves(1)
-        for n in range(2, GROUPS - 1):
-            load_x(n, 0, ROW_TILES, 0, K1)
-        load_x_halves(GROUPS - 1)
+        for n in range(1, GROUPS):
+            if n <= HALF_LOADS or n == GROUPS - 1:
+                load_x_halves(n)
+            else:
+                load_x(n, 0, ROW_TILES, 0, K1)
 
         gamma_z = const.tile([P, COLS], BF16)
         nc.scalar.dma_start(out=gamma_z[:], in_=gamma_o)
@@ -130,11 +131,14 @@ def tile_selfprojection_pa_t_kernel(
         wi_codes = const.tile([P, GROUPS_PER_BATCH * COLS], U32, align_bytes=64)
         wi_scales = const.tile([P, GROUPS_PER_BATCH * COLS], U8, align_bytes=64)
 
-        def quantise_weight(raw, grouped, codes, scales, blocks):
-            nc.vector.tensor_copy(
-                out=grouped[:].rearrange("p (c n t) -> p c n t", c=blocks, n=COLS, t=PACK),
-                in_=raw[:].rearrange("p (c t n) -> p c n t", c=blocks, t=PACK, n=COLS),
+        def regroup_weight(raw, grouped, lo, hi, engine_copy):
+            cols = slice(lo * PACK * COLS, hi * PACK * COLS)
+            engine_copy(
+                out=grouped[:, cols].rearrange("p (c n t) -> p c n t", c=hi - lo, n=COLS, t=PACK),
+                in_=raw[:, cols].rearrange("p (c t n) -> p c n t", c=hi - lo, t=PACK, n=COLS),
             )
+
+        def quantise_weight(grouped, codes, scales):
             nc.vector.quantize_mx(out=codes[:].bitcast(FP8X4), scales=scales[:], in_=grouped[:])
 
         y_codes = const.tile([P, GROUPS * COLS], U32, align_bytes=64)
@@ -152,7 +156,7 @@ def tile_selfprojection_pa_t_kernel(
         y_rounded_of = {}
         y_words_of = {}
         y_grouped_of = {}
-        warm_bank = yw_banks.tile([P, ROW_TILES * COLS], F32, name="yw")
+        warm_bank = y_banks.tile([P, ROW_TILES * COLS], F32, name="y_ps")
 
         def keep_warm():
             nc.tensor.matmul(out=warm_bank[:], lhsT=zeros[:, :P], rhs=zeros[:], start=True, stop=True)
@@ -249,11 +253,11 @@ def tile_selfprojection_pa_t_kernel(
                     )
             return y_ps
 
-        def round_last_pair(n, u, y_ps):
+        def round_last_pair(n, u, y_ps, engine_copy):
             if u == 0:
                 y_grouped_of[n] = y_stage.tile([P, COLS * PACK], BF16, name="y_grouped", align_bytes=64)
             tiles = y_grouped_of[n][:].rearrange("p (j u e) -> p u j e", j=COLS, u=PAIRS, e=2)
-            nc.scalar.copy(out=tiles[:, u], in_=y_ps[:].rearrange("p e j -> p j e"))
+            engine_copy(out=tiles[:, u], in_=y_ps[:].rearrange("p e j -> p j e"))
 
         def sum_last_group(n):
             b, g = divmod(n, GROUPS_PER_BATCH)
@@ -272,10 +276,7 @@ def tile_selfprojection_pa_t_kernel(
             nc.scalar.activation(out=sums[:], in_=y_ps[:], func=ACT.Copy, accum_out=c_parts[:, b, g : g + 1])
 
         def transpose_y_group(n):
-            if n < GROUPS - 2:
-                y_words = yw_banks.tile([P, PAIRS, COLS], F32, name="yw")
-            else:
-                y_words = xt_banks.tile([P, PAIRS, COLS], F32, name="xt")
+            y_words = xt_banks.tile([P, PAIRS, COLS], F32, name="xt")
             words = y_rounded_of[n][:].bitcast(F32)
             for u in range(PAIRS):
                 nc.tensor.transpose(y_words[:, u, :], words[:, u * P : (u + 1) * P], identity[:])
@@ -413,7 +414,8 @@ def tile_selfprojection_pa_t_kernel(
 
         for i in range(WARM_START):
             keep_warm()
-        quantise_weight(wj_raw, wj_grouped, wj_codes, wj_scales, PASSES_1)
+        regroup_weight(wj_raw, wj_grouped, 0, PASSES_1, nc.vector.tensor_copy)
+        quantise_weight(wj_grouped, wj_codes, wj_scales)
         for step in range(GROUPS):
             transpose_group(step)
             if started(step - 2):
@@ -423,7 +425,9 @@ def tile_selfprojection_pa_t_kernel(
                     quantise_pair(step - 1, u)
                 project_group(step - 1)
             if step == 1:
-                quantise_weight(wi_raw, wi_grouped, wi_codes, wi_scales, GROUPS_PER_BATCH)
+                regroup_weight(wi_raw, wi_grouped, 0, GROUPS_PER_BATCH // 2, nc.scalar.copy)
+                regroup_weight(wi_raw, wi_grouped, GROUPS_PER_BATCH // 2, GROUPS_PER_BATCH, nc.vector.tensor_copy)
+                quantise_weight(wi_grouped, wi_codes, wi_scales)
             if started(step - 3) and step < GROUPS - 1:
                 quantise_y_group(step - 3)
                 second_contraction(step - 3)
@@ -447,38 +451,38 @@ def tile_selfprojection_pa_t_kernel(
         transpose_y_group(end - 1)
         y_second = project_last_pair(end, 1)
         copy_y_group(end - 2, nc.scalar.copy)
-        round_last_pair(end, 0, y_first)
+        round_last_pair(end, 0, y_first, nc.scalar.copy)
         copy_y_group(end - 1, nc.scalar.copy)
-        round_last_pair(end, 1, y_second)
         quantise_y_group(end - 3)
-        quantise_y_group(end - 2)
         for b in range(half):
             z_spread_of(b)
+        quantise_y_group(end - 2)
+        round_last_pair(end, 1, y_second, nc.vector.tensor_copy)
         quantise_y_group(end - 1)
+        quantise_y_group(end)
         z_variance(0, half)
         sum_last_group(end)
         z_row_moments(last - 1)
-        quantise_y_group(end)
-        z_last = yw_banks.tile([P, COLS], F32, name="yw")
+        z_last = xt_banks.tile([P, COLS], F32, name="xt")
         z_of.append(z_last[:])
         for n in range(end - 3, end + 1):
             second_contraction(n)
-        for b in range(half):
-            z_centre(b)
-        c_to_rows()
+        z_centre(0)
         z_row_moments(last)
         z_mean(half, BATCH)
+        z_centre(1)
+        c_to_rows()
         z_reciprocal(0, half)
         for b in range(half):
             z_scale(b)
         z_store(0, half)
-        c_row_moments()
         for b in range(half, BATCH):
             z_spread_of(b)
-        c_moments()
         z_variance(half, BATCH)
-        for b in range(half, BATCH):
-            z_centre(b)
+        c_row_moments()
+        z_centre(half)
+        c_moments()
+        z_centre(last)
         c_centre()
         z_reciprocal(half, BATCH)
         for b in range(half, BATCH):

@@ -27,9 +27,9 @@ GROUPS = BATCH * GROUPS_PER_BATCH
 ROW_TILES = K_PASS // P
 WORDS = K1 // 2
 WORD_BLOCKS = WORDS // P
-HALF_LOADS = 3
+HALF_LOADS = 1
 WARM_START = 5
-WARM_GROUPS = 1
+WARM_GROUPS = 2
 BN_STATS = 6
 BN_AGGR = 2
 PAIRS = 2

@@ -98,13 +98,13 @@ def tile_selfprojection_pa_t_kernel(
                 load_x(n, 0, ROW_TILES, 0, K1)
 
         gamma_z = const.tile([P, COLS], BF16)
-        nc.scalar.dma_start(out=gamma_z[:], in_=gamma_o)
+        nc.sync.dma_start(out=gamma_z[:], in_=gamma_o)
         beta_z = const.tile([P, COLS], BF16)
-        nc.scalar.dma_start(out=beta_z[:], in_=beta_o)
+        nc.sync.dma_start(out=beta_z[:], in_=beta_o)
         gamma_c = const.tile([BATCH, COLS], BF16)
-        nc.scalar.dma_start(out=gamma_c[:], in_=gamma_o_sum.partition_broadcast(BATCH))
+        nc.sync.dma_start(out=gamma_c[:], in_=gamma_o_sum.partition_broadcast(BATCH))
         beta_c = const.tile([BATCH, COLS], BF16)
-        nc.scalar.dma_start(out=beta_c[:], in_=beta_o_sum.partition_broadcast(BATCH))
+        nc.sync.dma_start(out=beta_c[:], in_=beta_o_sum.partition_broadcast(BATCH))
 
         zeros = const.tile([P, ROW_TILES * COLS], BF16)
         nc.gpsimd.memset(zeros[:], 0.0)
@@ -118,8 +118,6 @@ def tile_selfprojection_pa_t_kernel(
         nc.gpsimd.tensor_tensor(out=centre[:], in0=identity[:], in1=average[:], op=ALU.subtract)
         c_columns = const.tile([P, P], F32)
         nc.gpsimd.memset(c_columns[:], 0.0)
-        beta_c_plus_1 = const.tile([BATCH, COLS], F32)
-        nc.gpsimd.tensor_scalar_add(out=beta_c_plus_1[:], in0=beta_c[:], scalar1=1.0)
 
         warm = const.tile([P, 1], F32)
         nc.scalar.activation(out=warm[:], in_=one[:], func=ACT.Sqrt)
@@ -146,6 +144,8 @@ def tile_selfprojection_pa_t_kernel(
         z_ps = z_bank.tile([P, BATCH - 1, COLS], F32)
         z_of = [z_ps[:, b, :] for b in range(BATCH - 1)]
         c_parts = const.tile([P, BATCH, GROUPS_PER_BATCH], F32)
+        beta_c_plus_1 = const.tile([BATCH, COLS], F32)
+        nc.gpsimd.tensor_scalar_add(out=beta_c_plus_1[:], in0=beta_c[:], scalar1=1.0)
         z_stats = const.tile([P, BATCH, BN_STATS], F32)
         z_mv = const.tile([P, BATCH, BN_AGGR], F32)
 
@@ -321,8 +321,10 @@ def tile_selfprojection_pa_t_kernel(
         mean_of = {}
         var_of = {}
 
-        def z_row_moments(b):
+        def z_row_sums(b):
             nc.vector.bn_stats(out=z_stats[:, b, :], in_=z_of[b])
+
+        def z_row_moments(b):
             nc.vector.bn_aggr(out=z_mv[:, b, :], in_=z_stats[:, b, :])
 
         def z_mean(lo, hi):
@@ -355,9 +357,12 @@ def tile_selfprojection_pa_t_kernel(
                 out=z_std[:, cols], in_=var_ps[:], func=ACT.Sqrt, scale=count_z / (count_z - 1.0)
             )
 
-        def z_reciprocal(lo, hi):
+        def z_divisor(lo, hi):
             cols = slice(lo, hi)
             nc.vector.tensor_scalar_add(out=z_rstd[:, cols], in0=z_std[:, cols], scalar1=EPS)
+
+        def z_reciprocal(lo, hi):
+            cols = slice(lo, hi)
             nc.vector.reciprocal(out=z_rstd[:, cols], in_=z_rstd[:, cols])
 
         def z_scale(b):
@@ -366,8 +371,8 @@ def tile_selfprojection_pa_t_kernel(
                 op0=ALU.mult, op1=ALU.add,
             )
 
-        def z_store(lo, hi):
-            nc.sync.dma_start(out=out_0[lo:hi].rearrange("b p n -> p b n"), in_=z_out[:, lo:hi, :])
+        def z_store(lo, hi, queue):
+            queue.dma_start(out=out_0[lo:hi].rearrange("b p n -> p b n"), in_=z_out[:, lo:hi, :])
 
         c_stats = const.tile([BATCH, BN_STATS], F32)
         c_mv = const.tile([BATCH, BN_AGGR], F32)
@@ -396,15 +401,17 @@ def tile_selfprojection_pa_t_kernel(
                 op0=ALU.subtract, op1=ALU.mult,
             )
 
-        def c_reciprocal():
+        def c_divisor():
             nc.vector.tensor_scalar_add(out=c_rstd[:], in0=c_std[:], scalar1=EPS)
+
+        def c_reciprocal():
             nc.vector.reciprocal(out=c_rstd[:], in_=c_rstd[:])
 
         def c_store():
             nc.vector.scalar_tensor_tensor(
                 out=c_out[:], in0=c_centred[:], scalar=c_rstd[:], in1=beta_c_plus_1[:], op0=ALU.mult, op1=ALU.add
             )
-            nc.scalar.dma_start(out=out_1, in_=c_out[:])
+            nc.sync.dma_start(out=out_1, in_=c_out[:])
 
         def started(n):
             return 0 <= n < GROUPS
@@ -440,6 +447,7 @@ def tile_selfprojection_pa_t_kernel(
             if started(step - 2) and step < GROUPS - 1:
                 copy_y_group(step - 2, nc.vector.tensor_copy)
             if batch_ending(step - 4) is not None and step < GROUPS - 1:
+                z_row_sums(batch_ending(step - 4))
                 z_row_moments(batch_ending(step - 4))
 
         end = GROUPS - 1
@@ -462,20 +470,23 @@ def tile_selfprojection_pa_t_kernel(
         quantise_y_group(end)
         z_variance(0, half)
         sum_last_group(end)
+        z_row_sums(last - 1)
         z_row_moments(last - 1)
         z_last = xt_banks.tile([P, COLS], F32, name="xt")
         z_of.append(z_last[:])
         for n in range(end - 3, end + 1):
             second_contraction(n)
+        z_row_sums(last)
         z_centre(0)
         z_row_moments(last)
         z_mean(half, BATCH)
+        z_divisor(0, half)
         z_centre(1)
-        c_to_rows()
         z_reciprocal(0, half)
+        c_to_rows()
         for b in range(half):
             z_scale(b)
-        z_store(0, half)
+        z_store(0, half, nc.sync)
         for b in range(half, BATCH):
             z_spread_of(b)
         z_variance(half, BATCH)
@@ -484,9 +495,12 @@ def tile_selfprojection_pa_t_kernel(
         c_moments()
         z_centre(last)
         c_centre()
+        z_divisor(half, BATCH)
+        c_divisor()
         z_reciprocal(half, BATCH)
-        for b in range(half, BATCH):
-            z_scale(b)
-        z_store(half, BATCH)
         c_reciprocal()
+        z_scale(last)
+        z_store(last, BATCH, nc.sync)
+        z_scale(half)
+        z_store(half, last, nc.scalar)
         c_store()

@@ -64,15 +64,14 @@ def tile_selfprojection_pa_t_kernel(
 
         def load_wi():
             nc.sync.dma_start(
-                out=wi_raw[:].rearrange("p (g f) -> p g f", g=GROUPS_PER_BATCH),
-                in_=original_xi_y.rearrange("(g p t) n -> p g (t n)", g=GROUPS_PER_BATCH, p=P, t=PACK),
+                out=wi_raw[:], in_=original_xi_y.rearrange("(p r) n -> p (r n)", p=P, r=GROUPS_PER_BATCH * PACK)
             )
 
         x_tiles = []
 
         def load_x(n, first_tile, tiles, first_col, cols):
             b, g = divmod(n, GROUPS_PER_BATCH)
-            rows = x[b].rearrange("(g p t) k -> g p t k", g=GROUPS_PER_BATCH, p=P, t=ROW_TILES)[g]
+            rows = x[b].rearrange("(p g t) k -> g p t k", g=GROUPS_PER_BATCH, p=P, t=ROW_TILES)[g]
             t = slice(first_tile, first_tile + tiles)
             k = slice(first_col, first_col + cols)
             nc.sync.dma_start(

from contextlib import ExitStack

import concourse.mybir as mybir
from concourse.masks import make_identity

F32 = mybir.dt.float32
BF16 = mybir.dt.bfloat16
U32 = mybir.dt.uint32
U8 = mybir.dt.uint8
FP8X4 = mybir.dt.float8_e4m3fn_x4
ALU = mybir.AluOpType
ACT = mybir.ActivationFunctionType

P = 128
PACK = 4
K_PASS = P * PACK

BATCH = 4
ROWS = 2048
K1 = 1024
COLS = 128
EPS = 1e-05

PASSES_1 = K1 // K_PASS
GROUPS_PER_BATCH = ROWS // K_PASS
GROUPS = BATCH * GROUPS_PER_BATCH
ROW_TILES = K_PASS // P
WORDS = K1 // 2
WORD_BLOCKS = WORDS // P
HALF_LOADS = 1
WARM_START = 5
WARM_GROUPS = 2
BN_STATS = 6
BN_AGGR = 2
PAIRS = 2
PAIR_COLS = ROW_TILES // PAIRS * P
Y_WORDS = K_PASS // 2

FLOPS = 2 * BATCH * ROWS * K1 * COLS + 2 * BATCH * COLS * ROWS * COLS


def tile_selfprojection_pa_t_kernel(
    tc, x, original_xj_y, original_xi_y, gamma_o_sum, gamma_o, beta_o_sum, beta_o, out_0, out_1
):
    nc = tc.nc
    with ExitStack() as ctx:
        ctx.enter_context(tc.manual_schedule())
        const = ctx.enter_context(tc.tile_pool(name="const", bufs=1))
        x_pool = ctx.enter_context(tc.tile_pool(name="x", bufs=GROUPS))
        stage = ctx.enter_context(tc.tile_pool(name="stage", bufs=3))
        y_stage = ctx.enter_context(tc.tile_pool(name="y_stage", bufs=3))
        xt_banks = ctx.enter_context(tc.psum_pool(name="xt_banks", bufs=6))
        y_banks = ctx.enter_context(tc.psum_pool(name="y_banks", bufs=1))
        z_bank = ctx.enter_context(tc.psum_pool(name="z_bank", bufs=1))

        wj_raw = const.tile([P, PASSES_1 * PACK * COLS], BF16)
        wi_raw = const.tile([P, GROUPS_PER_BATCH * PACK * COLS], BF16)

        def load_wj():
            nc.sync.dma_start(
                out=wj_raw[:].rearrange("p (h f) -> p h f", h=2 * PASSES_1),
                in_=original_xj_y.rearrange("(h p e) n -> p h (e n)", h=2 * PASSES_1, p=P, e=2),
            )

        def load_wi():
            nc.sync.dma_start(
                out=wi_raw[:], in_=original_xi_y.rearrange("(p r) n -> p (r n)", p=P, r=GROUPS_PER_BATCH * PACK)
            )

        x_tiles = []

        def load_x(n, first_tile, tiles, first_col, cols):
            b, g = divmod(n, GROUPS_PER_BATCH)
            rows = x[b].rearrange("(p g t) k -> g p t k", g=GROUPS_PER_BATCH, p=P, t=ROW_TILES)[g]
            t = slice(first_tile, first_tile + tiles)
            k = slice(first_col, first_col + cols)
            nc.sync.dma_start(
                out=x_tiles[n][:].rearrange("p (t k) -> p t k", t=ROW_TILES)[:, t, k], in_=rows[:, t, k]
            )

        def load_x_halves(n):
            for u in range(PAIRS):
                load_x(n, 2 * u, 2, 0, K1)

        for n in range(GROUPS):
            x_sb = x_pool.tile([P, ROW_TILES * K1], BF16, name="x_sb")
            x_tiles.append(x_sb)
        load_x(0, 0, 2, 0, K_PASS)
        load_x(0, 0, 2, K_PASS, K_PASS)
        load_wj()
        load_x(0, 2, 2, 0, K1)
        load_wi()
        for n in range(1, GROUPS):
            if n <= HALF_LOADS or n == GROUPS - 1:
                load_x_halves(n)
            else:
                load_x(n, 0, ROW_TILES, 0, K1)

        gamma_z = const.tile([P, COLS], BF16)
        nc.sync.dma_start(out=gamma_z[:], in_=gamma_o)
        beta_z = const.tile([P, COLS], BF16)
        nc.sync.dma_start(out=beta_z[:], in_=beta_o)
        gamma_c = const.tile([BATCH, COLS], BF16)
        nc.sync.dma_start(out=gamma_c[:], in_=gamma_o_sum.partition_broadcast(BATCH))
        beta_c = const.tile([BATCH, COLS], BF16)
        nc.sync.dma_start(out=beta_c[:], in_=beta_o_sum.partition_broadcast(BATCH))

        zeros = const.tile([P, ROW_TILES * COLS], BF16)
        nc.gpsimd.memset(zeros[:], 0.0)
        identity = const.tile([P, P], F32)
        make_identity(nc, identity[:])
        one = const.tile([P, 1], F32)
        nc.gpsimd.memset(one[:], 1.0)
        average = const.tile([P, P], F32)
        nc.gpsimd.memset(average[:], 1.0 / P)
        centre = const.tile([P, P], F32)
        nc.gpsimd.tensor_tensor(out=centre[:], in0=identity[:], in1=average[:], op=ALU.subtract)
        c_columns = const.tile([P, P], F32)
        nc.gpsimd.memset(c_columns[:], 0.0)

        warm = const.tile([P, 1], F32)
        nc.scalar.activation(out=warm[:], in_=one[:], func=ACT.Sqrt)

        wj_grouped = const.tile([P, PASSES_1 * COLS * PACK], BF16, align_bytes=64)
        wj_codes = const.tile([P, PASSES_1 * COLS], U32, align_bytes=64)
        wj_scales = const.tile([P, PASSES_1 * COLS], U8, align_bytes=64)
        wi_grouped = const.tile([P, GROUPS_PER_BATCH * COLS * PACK], BF16, align_bytes=64)
        wi_codes = const.tile([P, GROUPS_PER_BATCH * COLS], U32, align_bytes=64)
        wi_scales = const.tile([P, GROUPS_PER_BATCH * COLS], U8, align_bytes=64)

        def regroup_weight(raw, grouped, lo, hi, engine_copy):
            cols = slice(lo * PACK * COLS, hi * PACK * COLS)
            engine_copy(
                out=grouped[:, cols].rearrange("p (c n t) -> p c n t", c=hi - lo, n=COLS, t=PACK),
                in_=raw[:, cols].rearrange("p (c t n) -> p c n t", c=hi - lo, t=PACK, n=COLS),
            )

        def quantise_weight(grouped, codes, scales):
            nc.vector.quantize_mx(out=codes[:].bitcast(FP8X4), scales=scales[:], in_=grouped[:])

        y_codes = const.tile([P, GROUPS * COLS], U32, align_bytes=64)
        y_scales = const.tile([P, GROUPS * COLS], U8, align_bytes=64)
        z_ps = z_bank.tile([P, BATCH - 1, COLS], F32)
        z_of = [z_ps[:, b, :] for b in range(BATCH - 1)]
        c_parts = const.tile([P, BATCH, GROUPS_PER_BATCH], F32)
        beta_c_plus_1 = const.tile([BATCH, COLS], F32)
        nc.gpsimd.tensor_scalar_add(out=beta_c_plus_1[:], in0=beta_c[:], scalar1=1.0)
        z_stats = const.tile([P, BATCH, BN_STATS], F32)
        z_mv = const.tile([P, BATCH, BN_AGGR], F32)

        xt_of = {}
        grouped_of = {}
        codes_of = {}
        y_of = {}
        y_rounded_of = {}
        y_words_of = {}
        y_grouped_of = {}
        warm_bank = y_banks.tile([P, ROW_TILES * COLS], F32, name="y_ps")

        def keep_warm():
            nc.tensor.matmul(out=warm_bank[:], lhsT=zeros[:, :P], rhs=zeros[:], start=True, stop=True)

        def transpose_group(n):
            words = x_tiles[n][:].bitcast(F32)
            for u in range(PAIRS):
                for c in range(PASSES_1):
                    xt = xt_banks.tile([P, WORD_BLOCKS * P], F32, name="xt")
                    for e in range(ROW_TILES // PAIRS):
                        for w in range(WORD_BLOCKS // PASSES_1):
                            first = (2 * u + e) * WORDS + (2 * c + w) * P
                            slot = 2 * e + w
                            nc.tensor.transpose(
                                xt[:, slot * P : (slot + 1) * P], words[:, first : first + P], identity[:]
                            )
                    xt_of[n, u, c] = xt
                    if n < WARM_GROUPS:
                        keep_warm()

        def copy_bank(n, u, c, engine_copy):
            if (u, c) == (0, 0):
                grouped_of[n] = stage.tile(
                    [P, PAIRS * PASSES_1 * PAIR_COLS * PACK], BF16, name="grouped", align_bytes=64
                )
            words = grouped_of[n][:].bitcast(F32)
            bank = slice((u * PASSES_1 + c) * WORD_BLOCKS * P, (u * PASSES_1 + c + 1) * WORD_BLOCKS * P)
            xt = xt_of[n, u, c][:]
            if n == GROUPS - 1:
                engine_copy(
                    out=words[:, bank].rearrange("p (e m w) -> p e m w", e=2, m=P, w=2),
                    in_=xt.rearrange("p (e w m) -> p e m w", e=2, w=2, m=P),
                )
            else:
                engine_copy(
                    out=words[:, bank].rearrange("p (m s) -> p m s", m=P, s=WORD_BLOCKS),
                    in_=xt.rearrange("p (s m) -> p m s", s=WORD_BLOCKS, m=P),
                )

        def quantise_pair(n, u):
            width = PASSES_1 * PAIR_COLS
            if u == 0:
                codes_of[n] = (
                    stage.tile([P, PAIRS * width], U32, name="codes", align_bytes=64),
                    stage.tile([P, PAIRS * width], U8, name="scales", align_bytes=64),
                )
            codes, scales = codes_of[n]
            cols = slice(u * width, (u + 1) * width)
            nc.vector.quantize_mx(
                out=codes[:, cols].bitcast(FP8X4),
                scales=scales[:, cols],
                in_=grouped_of[n][:, u * width * PACK : (u + 1) * width * PACK],
            )

        def project(out, lhsT, lhsT_scale, rhs, rhs_scale, first, last_pass):
            nc.tensor.matmul_mx(
                out=out, lhsT=lhsT.bitcast(FP8X4), lhsT_scale=lhsT_scale, rhs=rhs.bitcast(FP8X4),
                rhs_scale=rhs_scale, start=first, stop=last_pass,
            )

        def project_group(n):
            codes, scales = codes_of[n]
            y_ps = y_banks.tile([P, PAIRS * PAIR_COLS], F32, name="y_ps")
            y_of[n] = y_ps
            for u in range(PAIRS):
                for c in range(PASSES_1):
                    first = (u * PASSES_1 + c) * PAIR_COLS
                    m_cols = slice(first, first + PAIR_COLS)
                    n_cols = slice(c * COLS, (c + 1) * COLS)
                    project(
                        y_ps[:, u * PAIR_COLS : (u + 1) * PAIR_COLS], wj_codes[:, n_cols], wj_scales[:, n_cols],
                        codes[:, m_cols], scales[:, m_cols], c == 0, c == PASSES_1 - 1,
                    )

        def round_group(n):
            b, g = divmod(n, GROUPS_PER_BATCH)
            y_rounded = y_stage.tile([P, K_PASS], BF16, name="y_rounded", align_bytes=64)
            nc.scalar.activation(
                out=y_rounded[:], in_=y_of[n][:], func=ACT.Copy, accum_out=c_parts[:, b, g : g + 1]
            )
            y_rounded_of[n] = y_rounded

        def project_last_pair(n, u):
            codes, scales = codes_of[n]
            y_ps = xt_banks.tile([P, ROW_TILES // PAIRS, COLS], F32, name="xt")
            for e in range(ROW_TILES // PAIRS):
                for c in range(PASSES_1):
                    first = ((u * PASSES_1 + c) * 2 + e) * P
                    m_cols = slice(first, first + P)
                    n_cols = slice(c * COLS, (c + 1) * COLS)
                    project(
                        y_ps[:, e, :], codes[:, m_cols], scales[:, m_cols], wj_codes[:, n_cols],
                        wj_scales[:, n_cols], c == 0, c == PASSES_1 - 1,
                    )
            return y_ps

        def round_last_pair(n, u, y_ps, engine_copy):
            if u == 0:
                y_grouped_of[n] = y_stage.tile([P, COLS * PACK], BF16, name="y_grouped", align_bytes=64)
            tiles = y_grouped_of[n][:].rearrange("p (j u e) -> p u j e", j=COLS, u=PAIRS, e=2)
            engine_copy(out=tiles[:, u], in_=y_ps[:].rearrange("p e j -> p j e"))

        def sum_last_group(n):
            b, g = divmod(n, GROUPS_PER_BATCH)
            codes, scales = codes_of[n]
            y_ps = y_banks.tile([P, PAIR_COLS], F32, name="y_ps")
            passes = [(u, c) for u in range(PAIRS) for c in range(PASSES_1)]
            for u, c in passes:
                first = (u * PASSES_1 + c) * PAIR_COLS
                m_cols = slice(first, first + PAIR_COLS)
                n_cols = slice(c * COLS, (c + 1) * COLS)
                project(
                    y_ps[:], wj_codes[:, n_cols], wj_scales[:, n_cols], codes[:, m_cols], scales[:, m_cols],
                    (u, c) == passes[0], (u, c) == passes[-1],
                )
            sums = y_stage.tile([P, PAIR_COLS], F32, name="sums")
            nc.scalar.activation(out=sums[:], in_=y_ps[:], func=ACT.Copy, accum_out=c_parts[:, b, g : g + 1])

        def transpose_y_group(n):
            y_words = xt_banks.tile([P, PAIRS, COLS], F32, name="xt")
            words = y_rounded_of[n][:].bitcast(F32)
            for u in range(PAIRS):
                nc.tensor.transpose(y_words[:, u, :], words[:, u * P : (u + 1) * P], identity[:])
            y_words_of[n] = y_words

        def copy_y_group(n, engine_copy):
            y_grouped = y_stage.tile([P, COLS * PACK], BF16, name="y_grouped", align_bytes=64)
            engine_copy(
                out=y_grouped[:].bitcast(F32).rearrange("p (j u) -> p j u", u=PAIRS),
                in_=y_words_of[n][:].rearrange("p u j -> p j u"),
            )
            y_grouped_of[n] = y_grouped

        def quantise_y_group(n):
            cols = slice(n * COLS, (n + 1) * COLS)
            nc.vector.quantize_mx(
                out=y_codes[:, cols].bitcast(FP8X4), scales=y_scales[:, cols], in_=y_grouped_of[n][:]
            )

        def second_contraction(n):
            b, g = divmod(n, GROUPS_PER_BATCH)
            i_cols = slice(g * COLS, (g + 1) * COLS)
            j_cols = slice(n * COLS, (n + 1) * COLS)
            nc.tensor.matmul_mx(
                out=z_of[b],
                lhsT=wi_codes[:, i_cols].bitcast(FP8X4),
                lhsT_scale=wi_scales[:, i_cols],
                rhs=y_codes[:, j_cols].bitcast(FP8X4),
                rhs_scale=y_scales[:, j_cols],
                start=(g == 0),
                stop=(g == GROUPS_PER_BATCH - 1),
            )

        last = BATCH - 1
        count_z = COLS * COLS
        z_spread = const.tile([P, BATCH], F32)
        z_std = const.tile([P, BATCH], F32)
        z_rstd = const.tile([P, BATCH], F32)
        centred = const.tile([P, BATCH, COLS], F32)
        z_out = const.tile([P, BATCH, COLS], F32)
        dev_of = {}
        mean_of = {}
        var_of = {}

        def z_row_sums(b):
            nc.vector.bn_stats(out=z_stats[:, b, :], in_=z_of[b])

        def z_row_moments(b):
            nc.vector.bn_aggr(out=z_mv[:, b, :], in_=z_stats[:, b, :])

        def z_mean(lo, hi):
            row_mean = z_mv[:, lo:hi, 0]
            dev_ps = xt_banks.tile([P, hi - lo], F32, name="xt")
            nc.tensor.matmul(out=dev_ps[:], lhsT=centre[:], rhs=row_mean, start=True, stop=True)
            mean_ps = xt_banks.tile([P, hi - lo], F32, name="xt")
            nc.tensor.matmul(out=mean_ps[:], lhsT=average[:], rhs=row_mean, start=True, stop=True)
            for b in range(lo, hi):
                dev_of[b] = dev_ps[:, b - lo : b - lo + 1]
                mean_of[b] = mean_ps[:, b - lo : b - lo + 1]

        def z_spread_of(b):
            nc.vector.scalar_tensor_tensor(
                out=z_spread[:, b : b + 1], in0=dev_of[b], scalar=dev_of[b], in1=z_mv[:, b, 1:2],
                op0=ALU.mult, op1=ALU.add,
            )

        def z_centre(b):
            nc.vector.scalar_tensor_tensor(
                out=centred[:, b, :], in0=z_of[b], scalar=mean_of[b], in1=gamma_z[:],
                op0=ALU.subtract, op1=ALU.mult,
            )

        def z_variance(lo, hi):
            cols = slice(lo, hi)
            var_ps = xt_banks.tile([P, hi - lo], F32, name="xt")
            nc.tensor.matmul(out=var_ps[:], lhsT=average[:], rhs=z_spread[:, cols], start=True, stop=True)
            nc.scalar.activation(
                out=z_std[:, cols], in_=var_ps[:], func=ACT.Sqrt, scale=count_z / (count_z - 1.0)
            )

        def z_divisor(lo, hi):
            cols = slice(lo, hi)
            nc.vector.tensor_scalar_add(out=z_rstd[:, cols], in0=z_std[:, cols], scalar1=EPS)

        def z_reciprocal(lo, hi):
            cols = slice(lo, hi)
            nc.vector.reciprocal(out=z_rstd[:, cols], in_=z_rstd[:, cols])

        def z_scale(b):
            nc.vector.scalar_tensor_tensor(
                out=z_out[:, b, :], in0=centred[:, b, :], scalar=z_rstd[:, b : b + 1], in1=beta_z[:],
                op0=ALU.mult, op1=ALU.add,
            )

        def z_store(lo, hi, queue):
            queue.dma_start(out=out_0[lo:hi].rearrange("b p n -> p b n"), in_=z_out[:, lo:hi, :])

        c_stats = const.tile([BATCH, BN_STATS], F32)
        c_mv = const.tile([BATCH, BN_AGGR], F32)
        c_std = const.tile([BATCH, 1], F32)
        c_rstd = const.tile([BATCH, 1], F32)
        c_centred = const.tile([BATCH, COLS], F32)
        c_out = const.tile([BATCH, COLS], F32)
        c_rows_of = {}

        def c_to_rows():
            nc.vector.tensor_reduce(out=c_columns[:, :BATCH], in_=c_parts[:], axis=mybir.AxisListType.X, op=ALU.add)
            c_ps = y_banks.tile([P, P], F32, name="y_ps")
            nc.tensor.transpose(c_ps[:], c_columns[:], identity[:])
            c_rows_of[0] = c_ps

        def c_row_moments():
            nc.vector.bn_stats(out=c_stats[:], in_=c_rows_of[0][:BATCH, :])

        def c_moments():
            nc.vector.bn_aggr(out=c_mv[:], in_=c_stats[:])
            nc.scalar.activation(out=c_std[:], in_=c_mv[:, 1:2], func=ACT.Sqrt, scale=COLS / (COLS - 1.0))

        def c_centre():
            nc.vector.scalar_tensor_tensor(
                out=c_centred[:], in0=c_rows_of[0][:BATCH, :], scalar=c_mv[:, 0:1], in1=gamma_c[:],
                op0=ALU.subtract, op1=ALU.mult,
            )

        def c_divisor():
            nc.vector.tensor_scalar_add(out=c_rstd[:], in0=c_std[:], scalar1=EPS)

        def c_reciprocal():
            nc.vector.reciprocal(out=c_rstd[:], in_=c_rstd[:])

        def c_store():
            nc.vector.scalar_tensor_tensor(
                out=c_out[:], in0=c_centred[:], scalar=c_rstd[:], in1=beta_c_plus_1[:], op0=ALU.mult, op1=ALU.add
            )
            nc.sync.dma_start(out=out_1, in_=c_out[:])

        def started(n):
            return 0 <= n < GROUPS

        def batch_ending(n):
            return n // GROUPS_PER_BATCH if started(n) and n % GROUPS_PER_BATCH == GROUPS_PER_BATCH - 1 else None

        for i in range(WARM_START):
            keep_warm()
        regroup_weight(wj_raw, wj_grouped, 0, PASSES_1, nc.vector.tensor_copy)
        quantise_weight(wj_grouped, wj_codes, wj_scales)
        for step in range(GROUPS):
            transpose_group(step)
            if started(step - 2):
                transpose_y_group(step - 2)
            if started(step - 1):
                for u in range(PAIRS):
                    quantise_pair(step - 1, u)
                project_group(step - 1)
            if step == 1:
                regroup_weight(wi_raw, wi_grouped, 0, GROUPS_PER_BATCH // 2, nc.scalar.copy)
                regroup_weight(wi_raw, wi_grouped, GROUPS_PER_BATCH // 2, GROUPS_PER_BATCH, nc.vector.tensor_copy)
                quantise_weight(wi_grouped, wi_codes, wi_scales)
            if started(step - 3) and step < GROUPS - 1:
                quantise_y_group(step - 3)
                second_contraction(step - 3)
            copy_bank(step, 0, 0, nc.scalar.copy)
            copy_bank(step, 0, 1, nc.scalar.copy)
            copy_bank(step, 1, 0, nc.vector.tensor_copy)
            copy_bank(step, 1, 1, nc.scalar.copy)
            if started(step - 1):
                round_group(step - 1)
            if started(step - 2) and step < GROUPS - 1:
                copy_y_group(step - 2, nc.vector.tensor_copy)
            if batch_ending(step - 4) is not None and step < GROUPS - 1:
                z_row_sums(batch_ending(step - 4))
                z_row_moments(batch_ending(step - 4))

        end = GROUPS - 1
        half = BATCH // 2
        z_mean(0, half)
        quantise_pair(end, 0)
        y_first = project_last_pair(end, 0)
        quantise_pair(end, 1)
        transpose_y_group(end - 1)
        y_second = project_last_pair(end, 1)
        copy_y_group(end - 2, nc.scalar.copy)
        round_last_pair(end, 0, y_first, nc.scalar.copy)
        copy_y_group(end - 1, nc.scalar.copy)
        quantise_y_group(end - 3)
        for b in range(half):
            z_spread_of(b)
        quantise_y_group(end - 2)
        round_last_pair(end, 1, y_second, nc.vector.tensor_copy)
        quantise_y_group(end - 1)
        quantise_y_group(end)
        z_variance(0, half)
        sum_last_group(end)
        z_row_sums(last - 1)
        z_row_moments(last - 1)
        z_last = xt_banks.tile([P, COLS], F32, name="xt")
        z_of.append(z_last[:])
        for n in range(end - 3, end + 1):
            second_contraction(n)
        z_row_sums(last)
        z_centre(0)
        z_row_moments(last)
        z_mean(half, BATCH)
        z_divisor(0, half)
        z_centre(1)
        z_reciprocal(0, half)
        c_to_rows()
        for b in range(half):
            z_scale(b)
        z_store(0, half, nc.sync)
        for b in range(half, BATCH):
            z_spread_of(b)
        z_variance(half, BATCH)
        c_row_moments()
        z_centre(half)
        c_moments()
        z_centre(last)
        c_centre()
        z_divisor(half, BATCH)
        c_divisor()
        z_reciprocal(half, BATCH)
        c_reciprocal()
        z_scale(last)
        z_store(last, BATCH, nc.sync)
        z_scale(half)
        z_store(half, last, nc.scalar)
        c_store()
